import numpy as np
import ml_dtypes


def mxq(x, axis, fmt="e4m3"):
    dtype, down = {"e4m3": (ml_dtypes.float8_e4m3fn, 7), "e5m2": (ml_dtypes.float8_e5m2, 14)}[fmt]
    v = np.moveaxis(np.asarray(x, np.float32).astype(ml_dtypes.bfloat16).astype(np.float64), axis, -1)
    blocks = v.reshape(v.shape[:-1] + (-1, 32))
    amax = np.abs(blocks).max(-1, keepdims=True)
    byte = np.maximum(np.where(amax > 0, np.frexp(amax)[1] - 1 + 127, 0) - down, 1)
    scale = np.exp2(byte - 127.0)
    codes = (blocks / scale).astype(np.float32).astype(dtype).astype(np.float64)
    return np.moveaxis((codes * scale).reshape(v.shape), -1, axis)


WIDE = False


def mx_kscale(k):
    if not WIDE:
        return np.ones(k)
    levels = np.array([10, -10, 5, -5, 0])
    if k % 512:
        return np.exp2(np.random.permutation(np.resize(levels, k // 32))).repeat(32)
    a = np.empty((k // 512, 16))
    for p in range(k // 512):
        a[p, :8] = np.random.permutation(np.resize(levels, 8))
        for g in range(8):
            far = levels[np.abs(levels - a[p, g]) >= 10]
            a[p, g + 8] = far[np.random.randint(len(far))]
    return np.exp2(a.ravel()).repeat(32)


BF16 = ml_dtypes.bfloat16


def bf(x):
    return np.asarray(x, np.float32).astype(BF16)


def f64(x):
    return np.asarray(x).astype(np.float64)


B, N, D = 4, 512, 512
C = 2 * D
EPS_BN = 1e-5
NEG_SLOPE = 0.01


def bn_lrelu(x, g, b):
    mean = np.mean(x, axis=(0, 2), keepdims=True)
    var = np.var(x, axis=(0, 2), keepdims=True)
    y = (x - mean) / np.sqrt(var + EPS_BN) * g[None, :, None] + b[None, :, None]
    return np.where(y >= 0, y, NEG_SLOPE * y)


def draw0():
    s = mx_kscale(C)
    v = np.random.standard_normal((B, C, N))
    return {"h1": bf(np.where(v >= 0, v, NEG_SLOPE * v) * s[None, :, None]),
            "W2": bf(np.random.standard_normal((D, C)) / np.sqrt(C) / s[None, :]),
            "g2": bf(1.0 + 0.2 * np.random.standard_normal(D)),
            "b2": bf(0.3 * np.random.standard_normal(D))}


def core(h1, W2, g2, b2):
    z = mxq(f64(W2), 1, "e4m3") @ mxq(f64(h1), 1, "e4m3")
    return np.swapaxes(bn_lrelu(z, f64(g2), f64(b2)), 1, 2)


def e4m3fn_bytes(y):
    return np.clip(np.asarray(y, np.float64), -448.0, 448.0).astype(np.float32).astype(ml_dtypes.float8_e4m3fn).view(np.uint8)


def e4m3fn_values(b):
    return np.asarray(b, np.uint8).view(ml_dtypes.float8_e4m3fn).astype(np.float64)


def setup_inputs():
    d = draw0()
    x0 = np.asarray(d['h1']).astype(np.float64)
    s = (np.max(np.abs(x0), axis=(0, 2), keepdims=True) / 448.0).astype(np.float32)
    out = {}
    for k, v in d.items():
        if k == 'h1':
            out['h1_bytes'] = e4m3fn_bytes(x0 / s.astype(np.float64))
            out['h1_scale'] = s
        else:
            out[k] = v
    return out


def reference(h1_bytes, h1_scale, W2, g2, b2):
    return core(e4m3fn_values(h1_bytes) * h1_scale.astype(np.float64), W2, g2, b2)

@@ -1,0 +1,271 @@
+from contextlib import ExitStack
+
+import concourse.mybir as mybir
+from concourse.masks import make_identity
+
+FLOPS = 2 * 512 * 1024 * 2048
+
+F32 = mybir.dt.float32
+BF16 = mybir.dt.bfloat16
+U32 = mybir.dt.uint32
+U8 = mybir.dt.uint8
+FP8 = mybir.dt.float8_e4m3fn
+FP8X4 = mybir.dt.float8_e4m3fn_x4
+ACT = mybir.ActivationFunctionType
+ALU = mybir.AluOpType
+
+P = 128
+NB = 4
+NN = 512
+NOT = 4
+NG = 2
+EPS = 1e-5
+SLOPE = 0.01
+
+S_INTERLEAVES = (6, 7)
+V_WIDENS = ((0, 2), (0, 3))
+
+
+def tile_yuyipointupdate_pb_kernel(tc, h1_bytes, h1_scale, W2, g2, b2, out):
+    nc = tc.nc
+    with ExitStack() as ctx:
+        const = ctx.enter_context(tc.tile_pool(name="const", bufs=1))
+        keep = ctx.enter_context(tc.tile_pool(name="keep", bufs=1))
+        grp_pool = ctx.enter_context(tc.tile_pool(name="grp", bufs=3))
+        yr_pool = ctx.enter_context(tc.tile_pool(name="yr", bufs=4))
+        o_pool = ctx.enter_context(tc.tile_pool(name="osb", bufs=4))
+        psum = ctx.enter_context(tc.psum_pool(name="psum", bufs=4))
+        ctx.enter_context(tc.manual_schedule())
+
+        hscale = const.tile([P, NG, 8], F32, name="hscale")
+        nc.sync.dma_start(
+            out=hscale[:, :, 0:4],
+            in_=h1_scale.rearrange("a k u -> (a k u)").rearrange("(g p t) -> p g t", p=P, t=4),
+        )
+        hb = []
+        for c in range(8):
+            hb.append(keep.tile([P, 4, NN], U8, name="hbytes%d" % c))
+        wraw = []
+        for ot in range(NOT):
+            wraw.append(keep.tile([P, 1024], BF16, name="wraw%d" % ot))
+
+        def load_h(c):
+            b, g = c // 2, c % 2
+            nc.sync.dma_start(out=hb[c][:], in_=h1_bytes[b].rearrange("(g p t) n -> g p t n", p=P, t=4)[g])
+
+        load_h(0)
+        load_h(1)
+        for ot in range(NOT):
+            nc.sync.dma_start(out=wraw[ot][:], in_=W2[ot * P:(ot + 1) * P, :])
+        for c in range(2, 8):
+            load_h(c)
+        g2raw = const.tile([P, NOT, 1], BF16, name="g2raw")
+        b2raw = const.tile([P, NOT, 1], BF16, name="b2raw")
+        with nc.allow_non_contiguous_dma(reason="512 gains and shifts, one to a partition and tile"):
+            nc.sync.dma_start(out=g2raw[:].rearrange("p t u -> p (t u)"), in_=g2.rearrange("(t p) -> p t", p=P))
+            nc.sync.dma_start(out=b2raw[:].rearrange("p t u -> p (t u)"), in_=b2.rearrange("(t p) -> p t", p=P))
+
+        one = const.tile([P, 1], F32, name="one")
+        nc.vector.memset(one[:], 1.0)
+        warm = const.tile([P, 1], F32, name="warm")
+        nc.scalar.activation(out=warm[:], in_=one[:], func=ACT.Sqrt)
+        ident = const.tile([P, P], F32, name="ident")
+        make_identity(nc, ident[:])
+        g2f = const.tile([P, NOT, 1], F32, name="g2f")
+        b2f = const.tile([P, NOT, 1], F32, name="b2f")
+        nc.gpsimd.tensor_copy(out=g2f[:], in_=g2raw[:])
+        nc.gpsimd.tensor_copy(out=b2f[:], in_=b2raw[:])
+
+        planes = []
+        hcod = []
+        hscl = []
+        for c in range(8):
+            planes.append(keep.tile([P, 4, NN], BF16, name="planes%d" % c))
+            hcod.append(keep.tile([P, NN], U32, name="hcod%d" % c, align_bytes=64))
+            hscl.append(keep.tile([P, NN], U8, name="hscl%d" % c, align_bytes=64))
+        wgrp = []
+        wcod = []
+        wscl = []
+        for g in range(NG):
+            wgrp.append(keep.tile([P, 2048], BF16, name="wgrp%d" % g, align_bytes=64))
+            wcod.append(keep.tile([P, 512], U32, name="wcod%d" % g, align_bytes=64))
+            wscl.append(keep.tile([P, 512], U8, name="wscl%d" % g, align_bytes=64))
+        stats = const.tile([P, NOT, NB, 6], F32, name="stats")
+        mv = const.tile([P, NOT, 2], F32, name="mv")
+        grp = {}
+        xt = {}
+        z = {}
+
+        def widen(c):
+            g = c % 2
+            for t in range(4):
+                src = hb[c][:, t, :].bitcast(FP8)
+                dst = planes[c][:, t, :]
+                sc = hscale[:, g, t:t + 1]
+                if (c, t) in V_WIDENS:
+                    nc.vector.tensor_scalar(out=dst, in0=src, scalar1=sc, scalar2=None, op0=ALU.mult)
+                else:
+                    nc.scalar.activation(out=dst, in_=src, func=ACT.Copy, scale=sc)
+
+        def interleave(c):
+            grp[c] = grp_pool.tile([P, 4 * NN], BF16, name="grp%d" % c, tag="grp", align_bytes=64)
+            dst = grp[c][:].rearrange("p (n t) -> p n t", t=4)
+            src = planes[c][:].rearrange("p t n -> p n t")
+            if c in S_INTERLEAVES:
+                nc.scalar.copy(out=dst, in_=src)
+            else:
+                nc.vector.tensor_copy(out=dst, in_=src)
+
+        def quantize(c):
+            nc.vector.quantize_mx(out=hcod[c][:].bitcast(FP8X4), scales=hscl[c][:], in_=grp[c][:])
+
+        def w_transposes(h):
+            for g in range(NG):
+                xt[(h, g)] = psum.tile([P, 2, 256], F32, name="xt%d%d" % (h, g), tag="z")
+                for u in range(2):
+                    for otl in range(2):
+                        words = wraw[2 * h + otl][:].bitcast(F32)
+                        nc.tensor.transpose(
+                            xt[(h, g)][:, u, otl * P:(otl + 1) * P],
+                            words[:, 256 * g + u:256 * (g + 1):2],
+                            ident[:],
+                        )
+
+        def w_evac(h, g):
+            nc.vector.tensor_copy(
+                out=wgrp[g][:].bitcast(F32)[:, h * 512:(h + 1) * 512].rearrange("p (r u) -> p r u", u=2),
+                in_=xt[(h, g)][:].rearrange("p u r -> p r u"),
+            )
+
+        def w_quantize(g):
+            nc.vector.quantize_mx(out=wcod[g][:].bitcast(FP8X4), scales=wscl[g][:], in_=wgrp[g][:])
+
+        def mx(acc, ot, c):
+            g = c % 2
+            cols = slice(ot * P, (ot + 1) * P)
+            nc.tensor.matmul_mx(
+                out=acc[:],
+                lhsT=wcod[g][:, cols].bitcast(FP8X4),
+                lhsT_scale=wscl[g][:, cols],
+                rhs=hcod[c][:].bitcast(FP8X4),
+                rhs_scale=hscl[c][:],
+                start=(g == 0),
+                stop=(g == 1),
+            )
+
+        def matmuls(c):
+            b, g = c // 2, c % 2
+            for ot in range(NOT):
+                if g == 0:
+                    z[(b, ot)] = psum.tile([P, NN], F32, name="z%d%d" % (b, ot), tag=("t" if b % 2 == 0 else "z"))
+                mx(z[(b, ot)], ot, c)
+
+        def bn(b, ot):
+            nc.vector.bn_stats(out=stats[:, ot, b, :], in_=z[(b, ot)][:])
+
+        widen(0)
+        w_transposes(0)
+        w_transposes(1)
+        widen(1)
+        interleave(0)
+        quantize(0)
+        widen(2)
+        interleave(1)
+        for h in range(2):
+            for g in range(NG):
+                w_evac(h, g)
+        w_quantize(0)
+        quantize(1)
+        w_quantize(1)
+        matmuls(0)
+        matmuls(1)
+        todo = [(b, ot) for b in range(3) for ot in range(NOT)]
+        for c in range(2, 8):
+            if c + 1 < 8:
+                widen(c + 1)
+            interleave(c)
+            if c > 2:
+                matmuls(c - 1)
+            bn(*todo[2 * (c - 2)])
+            quantize(c)
+            bn(*todo[2 * (c - 2) + 1])
+        matmuls(7)
+        for ot in range(NOT):
+            bn(3, ot)
+
+        for ot in range(NOT):
+            nc.vector.bn_aggr(out=mv[:, ot, :], in_=stats[:, ot, :, :].rearrange("p b s -> p (b s)"))
+        sd = const.tile([P, NOT, 1], F32, name="sd")
+        rstd = const.tile([P, NOT, 1], F32, name="rstd")
+        gain = const.tile([P, NOT, 1], F32, name="gain")
+        nmg = const.tile([P, NOT, 1], F32, name="nmg")
+        shift = const.tile([P, NOT, 1], F32, name="shift")
+        nc.scalar.activation(out=sd[:], in_=mv[:, :, 1:2], func=ACT.Sqrt, bias=EPS, scale=1.0)
+        nc.vector.reciprocal(out=rstd[:], in_=sd[:])
+        nc.vector.tensor_tensor(out=gain[:], in0=g2f[:], in1=rstd[:], op=ALU.mult)
+        nc.vector.scalar_tensor_tensor(out=nmg[:], in0=mv[:, :, 0:1], scalar=-1.0, in1=gain[:], op0=ALU.mult, op1=ALU.mult)
+        nc.vector.tensor_tensor(out=shift[:], in0=nmg[:], in1=b2f[:], op=ALU.add)
+
+        items = [(b, ot) for b in (2, 3, 0, 1) for ot in range(NOT)]
+        y = {}
+        r = {}
+        pt = {}
+        osb = {}
+
+        def recompute(i):
+            b, ot = items[i]
+            z[(b, ot)] = psum.tile([P, NN], F32, name="zz%d%d" % (b, ot), tag="z")
+            mx(z[(b, ot)], ot, 2 * b)
+            mx(z[(b, ot)], ot, 2 * b + 1)
+
+        def norm(i):
+            b, ot = items[i]
+            y[i] = yr_pool.tile([P, NN], F32, name="y%d" % i, tag="y")
+            nc.scalar.activation(out=y[i][:], in_=z[(b, ot)][:], func=ACT.Identity, bias=shift[:, ot, :], scale=gain[:, ot, :])
+
+        def leaky(i):
+            r[i] = yr_pool.tile([P, NN], F32, name="r%d" % i, tag="r")
+            nc.vector.scalar_tensor_tensor(out=r[i][:], in0=y[i][:], scalar=SLOPE, in1=y[i][:], op0=ALU.mult, op1=ALU.max)
+
+        def turn(i):
+            pt[i] = psum.tile([P, NN], F32, name="pt%d" % i, tag="t")
+            for j in range(4):
+                nc.tensor.transpose(pt[i][:, j * P:(j + 1) * P], r[i][:, j * P:(j + 1) * P], ident[:])
+
+        def evac(i):
+            k, otl = i // 2, i % 2
+            if otl == 0:
+                osb[k] = o_pool.tile([P, 4, 256], F32, name="osb%d" % k, tag="osb")
+            dst = osb[k][:, :, otl * P:(otl + 1) * P]
+            src = pt[i][:].rearrange("p (j o) -> p j o", j=4)
+            if otl == 0:
+                nc.scalar.copy(out=dst, in_=src)
+            else:
+                nc.vector.tensor_copy(out=dst, in_=src)
+
+        def store(k):
+            b, ot = items[2 * k]
+            nc.sync.dma_start(
+                out=out[b].rearrange("(j p) o -> p j o", p=P)[:, :, ot * P:(ot + 2) * P],
+                in_=osb[k][:],
+            )
+
+        for m in range(10):
+            done = 2 * m - 4
+            if 0 <= done < 16:
+                evac(done)
+            if 2 * m < 16:
+                norm(2 * m)
+                norm(2 * m + 1)
+            if 8 <= 2 * m + 4 < 16:
+                recompute(2 * m + 4)
+                recompute(2 * m + 5)
+            if 0 <= done < 16:
+                evac(done + 1)
+            if 2 * m < 16:
+                leaky(2 * m)
+                leaky(2 * m + 1)
+                turn(2 * m)
+                turn(2 * m + 1)
+            if 0 <= done < 16:
+                store(m - 2)

@@ -23,6 +23,27 @@ EPS = 1e-5
 SLOPE = 0.01
 
 S_INTERLEAVES = (6, 7)
+V_EVACS = (3, 5, 7, 9, 11, 13, 15)
+ORDER = (
+    "w0_0 w0_2 w0_1 w0_3 w1_0 I0 w1_1 X0_0 X0_1 X0_2 w1_2 X0_3 X0_4 X0_5 "
+    "X0_6 WE0_0 w1_3 X0_7 X1_0 X1_1 Q0 X1_2 X1_3 X1_4 w2_0 X1_5 WE0_1 X1_6 "
+    "X1_7 w2_1 WE1_0 w2_2 WE1_1 w2_3 QW0 w3_0 QW1 Ma0_0 w3_1 I1 Ma0_1 w3_2 "
+    "Ma0_2 Ma0_3 w3_3 I2 w4_0 w4_1 Q1 w4_2 w4_3 Q2 Mb0_0 w5_0 I3 Mb0_1 "
+    "Mb0_2 w5_1 Mb0_3 Ma1_0 w5_2 Ma1_1 BN0_0 Ma1_2 w5_3 Ma1_3 Q3 w6_0 BN0_1 w6_1 "
+    "Mb1_0 BN0_2 Mb1_1 w6_2 Mb1_2 BN0_3 Mb1_3 w6_3 I4 I6 I5 Q4 w7_0 Q5 "
+    "w7_1 Ma2_0 BN1_0 Ma2_1 w7_2 Ma2_2 BN1_1 Ma2_3 w7_3 Mb2_0 BN1_2 Mb2_1 I7 Mb2_2 "
+    "BN1_3 Mb2_3 Q6 BN2_0 Ma3_0 BN2_1 Ma3_1 Ma3_2 R0 Ma3_3 Q7 R1 BN2_2 R2 "
+    "Mb3_0 BN2_3 Mb3_1 R3 Mb3_2 BN3_0 Mb3_3 BN3_1 BN3_2 BN3_3 AG0 AG1 AG2 AG3 "
+    "SQ P0 P1 P2 P3 N0 L0 N4 N1 N5 L1 Ta0 Tb0 N6 "
+    "T0 Ma8 N2 L2 E0 Ta1 Tb1 N3 N7 T1 L3 Ta2 Tb2 T2 "
+    "E1 Ma9 L4 E2 Ta3 L5 ST0 Tb3 N8 T3 L6 Ta4 Tb4 N9 "
+    "T4 Ta5 E3 Tb5 T5 Ma10 E4 E5 ST1 Ma11 L7 N10 Ta6 L8 "
+    "Tb6 N11 T6 ST2 Ta7 Tb7 L9 T7 Ma12 E6 E7 Ma13 L10 N12 "
+    "Ta8 ST3 Tb8 L11 N13 T8 Ta9 Tb9 T9 Ma14 L12 E8 E9 Ma15 "
+    "N14 L13 Ta10 ST4 Tb10 N15 T10 Ta11 Tb11 L14 T11 Ta12 E10 Tb12 "
+    "T12 E11 E12 L15 Ta13 Tb13 T13 ST5 Ta14 Tb14 T14 E13 Ta15 Tb15 "
+    "E14 T15 ST6 SA14 EA15 EB15 SB15 SC15 "
+)
 V_WIDENS = ((0, 2), (0, 3))
 
 
@@ -31,7 +52,7 @@ def tile_yuyipointupdate_pb_kernel(tc, h1_bytes, h1_scale, W2, g2, b2, out):
     with ExitStack() as ctx:
         const = ctx.enter_context(tc.tile_pool(name="const", bufs=1))
         keep = ctx.enter_context(tc.tile_pool(name="keep", bufs=1))
-        grp_pool = ctx.enter_context(tc.tile_pool(name="grp", bufs=3))
+        grp_pool = ctx.enter_context(tc.tile_pool(name="grp", bufs=4))
         yr_pool = ctx.enter_context(tc.tile_pool(name="yr", bufs=4))
         o_pool = ctx.enter_context(tc.tile_pool(name="osb", bufs=4))
         psum = ctx.enter_context(tc.psum_pool(name="psum", bufs=4))
@@ -96,16 +117,30 @@ def tile_yuyipointupdate_pb_kernel(tc, h1_bytes, h1_scale, W2, g2, b2, out):
         xt = {}
         z = {}
 
-        def widen(c):
+        items = [(b, ot) for b in (2, 3, 0, 1) for ot in range(NOT)]
+        y = {}
+        r = {}
+        pt = {}
+        osb = {}
+        zs = {}
+        sd = const.tile([P, NOT, 1], F32, name="sd")
+        rstd = const.tile([P, NOT, 1], F32, name="rstd")
+        gain = const.tile([P, NOT, 1], F32, name="gain")
+        nmg = const.tile([P, NOT, 1], F32, name="nmg")
+        shift = const.tile([P, NOT, 1], F32, name="shift")
+
+        def bank(name, tag):
+            return psum.tile([P, NN], F32, name=name, tag=tag, bufs={"A": 3, "B": 1, "Z": 4}[tag])
+
+        def widen(c, t):
             g = c % 2
-            for t in range(4):
-                src = hb[c][:, t, :].bitcast(FP8)
-                dst = planes[c][:, t, :]
-                sc = hscale[:, g, t:t + 1]
-                if (c, t) in V_WIDENS:
-                    nc.vector.tensor_scalar(out=dst, in0=src, scalar1=sc, scalar2=None, op0=ALU.mult)
-                else:
-                    nc.scalar.activation(out=dst, in_=src, func=ACT.Copy, scale=sc)
+            src = hb[c][:, t, :].bitcast(FP8)
+            dst = planes[c][:, t, :]
+            sc = hscale[:, g, t:t + 1]
+            if (c, t) in V_WIDENS:
+                nc.vector.tensor_scalar(out=dst, in0=src, scalar1=sc, scalar2=None, op0=ALU.mult)
+            else:
+                nc.scalar.activation(out=dst, in_=src, func=ACT.Copy, scale=sc)
 
         def interleave(c):
             grp[c] = grp_pool.tile([P, 4 * NN], BF16, name="grp%d" % c, tag="grp", align_bytes=64)
@@ -119,22 +154,21 @@ def tile_yuyipointupdate_pb_kernel(tc, h1_bytes, h1_scale, W2, g2, b2, out):
         def quantize(c):
             nc.vector.quantize_mx(out=hcod[c][:].bitcast(FP8X4), scales=hscl[c][:], in_=grp[c][:])
 
-        def w_transposes(h):
-            for g in range(NG):
-                xt[(h, g)] = psum.tile([P, 2, 256], F32, name="xt%d%d" % (h, g), tag="z")
-                for u in range(2):
-                    for otl in range(2):
-                        words = wraw[2 * h + otl][:].bitcast(F32)
-                        nc.tensor.transpose(
-                            xt[(h, g)][:, u, otl * P:(otl + 1) * P],
-                            words[:, 256 * g + u:256 * (g + 1):2],
-                            ident[:],
-                        )
+        def w_transpose(h, k):
+            g, u, otl = k // 4, (k % 4) // 2, k % 2
+            if k % 4 == 0:
+                xt[(h, g)] = bank("xt%d%d" % (h, g), "Z")
+            words = wraw[2 * h + otl][:].bitcast(F32)
+            nc.tensor.transpose(
+                xt[(h, g)][:, u * 256 + otl * P:u * 256 + (otl + 1) * P],
+                words[:, 256 * g + u:256 * (g + 1):2],
+                ident[:],
+            )
 
         def w_evac(h, g):
             nc.vector.tensor_copy(
                 out=wgrp[g][:].bitcast(F32)[:, h * 512:(h + 1) * 512].rearrange("p (r u) -> p r u", u=2),
-                in_=xt[(h, g)][:].rearrange("p u r -> p r u"),
+                in_=xt[(h, g)][:].rearrange("p (u r) -> p r u", u=2),
             )
 
         def w_quantize(g):
@@ -153,95 +187,91 @@ def tile_yuyipointupdate_pb_kernel(tc, h1_bytes, h1_scale, W2, g2, b2, out):
                 stop=(g == 1),
             )
 
-        def matmuls(c):
-            b, g = c // 2, c % 2
-            for ot in range(NOT):
-                if g == 0:
-                    z[(b, ot)] = psum.tile([P, NN], F32, name="z%d%d" % (b, ot), tag=("t" if b % 2 == 0 else "z"))
-                mx(z[(b, ot)], ot, c)
+        def sweep_a(b, ot):
+            if b % 2 == 1:
+                tag = "Z"
+            else:
+                tag = "A" if ot < 3 else "B"
+            z[(b, ot)] = bank("z%d%d" % (b, ot), tag)
+            mx(z[(b, ot)], ot, 2 * b)
+
+        def sweep_b(b, ot):
+            mx(z[(b, ot)], ot, 2 * b + 1)
 
         def bn(b, ot):
             nc.vector.bn_stats(out=stats[:, ot, b, :], in_=z[(b, ot)][:])
 
-        widen(0)
-        w_transposes(0)
-        w_transposes(1)
-        widen(1)
-        interleave(0)
-        quantize(0)
-        widen(2)
-        interleave(1)
-        for h in range(2):
-            for g in range(NG):
-                w_evac(h, g)
-        w_quantize(0)
-        quantize(1)
-        w_quantize(1)
-        matmuls(0)
-        matmuls(1)
-        todo = [(b, ot) for b in range(3) for ot in range(NOT)]
-        for c in range(2, 8):
-            if c + 1 < 8:
-                widen(c + 1)
-            interleave(c)
-            if c > 2:
-                matmuls(c - 1)
-            bn(*todo[2 * (c - 2)])
-            quantize(c)
-            bn(*todo[2 * (c - 2) + 1])
-        matmuls(7)
-        for ot in range(NOT):
-            bn(3, ot)
-
-        for ot in range(NOT):
+        def aggr(ot):
             nc.vector.bn_aggr(out=mv[:, ot, :], in_=stats[:, ot, :, :].rearrange("p b s -> p (b s)"))
-        sd = const.tile([P, NOT, 1], F32, name="sd")
-        rstd = const.tile([P, NOT, 1], F32, name="rstd")
-        gain = const.tile([P, NOT, 1], F32, name="gain")
-        nmg = const.tile([P, NOT, 1], F32, name="nmg")
-        shift = const.tile([P, NOT, 1], F32, name="shift")
-        nc.scalar.activation(out=sd[:], in_=mv[:, :, 1:2], func=ACT.Sqrt, bias=EPS, scale=1.0)
-        nc.vector.reciprocal(out=rstd[:], in_=sd[:])
-        nc.vector.tensor_tensor(out=gain[:], in0=g2f[:], in1=rstd[:], op=ALU.mult)
-        nc.vector.scalar_tensor_tensor(out=nmg[:], in0=mv[:, :, 0:1], scalar=-1.0, in1=gain[:], op0=ALU.mult, op1=ALU.mult)
-        nc.vector.tensor_tensor(out=shift[:], in0=nmg[:], in1=b2f[:], op=ALU.add)
 
-        items = [(b, ot) for b in (2, 3, 0, 1) for ot in range(NOT)]
-        y = {}
-        r = {}
-        pt = {}
-        osb = {}
+        def root():
+            nc.scalar.activation(out=sd[:], in_=mv[:, :, 1:2], func=ACT.Sqrt, bias=EPS, scale=1.0)
+
+        def param(k):
+            if k == 0:
+                nc.vector.reciprocal(out=rstd[:], in_=sd[:])
+            elif k == 1:
+                nc.vector.tensor_tensor(out=gain[:], in0=g2f[:], in1=rstd[:], op=ALU.mult)
+            elif k == 2:
+                nc.vector.scalar_tensor_tensor(out=nmg[:], in0=mv[:, :, 0:1], scalar=-1.0, in1=gain[:], op0=ALU.mult, op1=ALU.mult)
+            else:
+                nc.vector.tensor_tensor(out=shift[:], in0=nmg[:], in1=b2f[:], op=ALU.add)
+
+        def raw(i):
+            zs[i] = keep.tile([P, NN], F32, name="zs%d" % i)
+            nc.scalar.copy(out=zs[i][:], in_=z[items[i]][:])
 
         def recompute(i):
             b, ot = items[i]
-            z[(b, ot)] = psum.tile([P, NN], F32, name="zz%d%d" % (b, ot), tag="z")
+            z[(b, ot)] = bank("zz%d%d" % (b, ot), "B" if i in (8, 13) else "Z")
             mx(z[(b, ot)], ot, 2 * b)
             mx(z[(b, ot)], ot, 2 * b + 1)
 
         def norm(i):
             b, ot = items[i]
-            y[i] = yr_pool.tile([P, NN], F32, name="y%d" % i, tag="y")
-            nc.scalar.activation(out=y[i][:], in_=z[(b, ot)][:], func=ACT.Identity, bias=shift[:, ot, :], scale=gain[:, ot, :])
+            y[i] = yr_pool.tile([P, NN], F32, name="y%d" % i, tag="y", bufs=8)
+            if i < 4:
+                nc.vector.tensor_scalar(out=y[i][:], in0=zs[i][:], scalar1=gain[:, ot, :], scalar2=shift[:, ot, :], op0=ALU.mult, op1=ALU.add)
+            else:
+                nc.scalar.activation(out=y[i][:], in_=z[(b, ot)][:], func=ACT.Identity, bias=shift[:, ot, :], scale=gain[:, ot, :])
 
         def leaky(i):
-            r[i] = yr_pool.tile([P, NN], F32, name="r%d" % i, tag="r")
+            r[i] = yr_pool.tile([P, NN], F32, name="r%d" % i, tag="r", bufs=6)
             nc.vector.scalar_tensor_tensor(out=r[i][:], in0=y[i][:], scalar=SLOPE, in1=y[i][:], op0=ALU.mult, op1=ALU.max)
 
-        def turn(i):
-            pt[i] = psum.tile([P, NN], F32, name="pt%d" % i, tag="t")
-            for j in range(4):
+        def turn(i, js):
+            if 0 in js:
+                pt[i] = bank("pt%d" % i, "A")
+            for j in js:
                 nc.tensor.transpose(pt[i][:, j * P:(j + 1) * P], r[i][:, j * P:(j + 1) * P], ident[:])
 
         def evac(i):
             k, otl = i // 2, i % 2
-            if otl == 0:
+            if k not in osb:
                 osb[k] = o_pool.tile([P, 4, 256], F32, name="osb%d" % k, tag="osb")
             dst = osb[k][:, :, otl * P:(otl + 1) * P]
             src = pt[i][:].rearrange("p (j o) -> p j o", j=4)
-            if otl == 0:
-                nc.scalar.copy(out=dst, in_=src)
-            else:
+            if i in V_EVACS:
                 nc.vector.tensor_copy(out=dst, in_=src)
+            else:
+                nc.scalar.copy(out=dst, in_=src)
+
+        def evac_part(i, j0, j1, on_vector):
+            k, otl = i // 2, i % 2
+            dst = osb[k][:, j0:j1, otl * P:(otl + 1) * P]
+            src = pt[i][:, j0 * P:j1 * P].rearrange("p (j o) -> p j o", j=j1 - j0)
+            if on_vector:
+                nc.vector.tensor_copy(out=dst, in_=src)
+            else:
+                nc.scalar.copy(out=dst, in_=src)
+
+        def store_part(i, j0, j1):
+            k, otl = i // 2, i % 2
+            b, ot = items[i]
+            nc.sync.dma_start(
+                out=out[b].rearrange("(j p) o -> p j o", p=P)[:, j0:j1, ot * P:(ot + 1) * P],
+                in_=osb[k][:, j0:j1, otl * P:(otl + 1) * P],
+            )
 
         def store(k):
             b, ot = items[2 * k]
@@ -250,22 +280,65 @@ def tile_yuyipointupdate_pb_kernel(tc, h1_bytes, h1_scale, W2, g2, b2, out):
                 in_=osb[k][:],
             )
 
-        for m in range(10):
-            done = 2 * m - 4
-            if 0 <= done < 16:
-                evac(done)
-            if 2 * m < 16:
-                norm(2 * m)
-                norm(2 * m + 1)
-            if 8 <= 2 * m + 4 < 16:
-                recompute(2 * m + 4)
-                recompute(2 * m + 5)
-            if 0 <= done < 16:
-                evac(done + 1)
-            if 2 * m < 16:
-                leaky(2 * m)
-                leaky(2 * m + 1)
-                turn(2 * m)
-                turn(2 * m + 1)
-            if 0 <= done < 16:
-                store(m - 2)
+        for tok in ORDER.split():
+            name = tok
+            args = []
+            for kind in ("SA", "SB", "SC", "EA", "EB", "Ma", "Mb", "BN", "WE", "QW", "AG", "SQ", "ST", "Ta", "Tb", "w", "I", "Q", "X", "P", "R", "N", "L", "T", "E"):
+                if tok.startswith(kind):
+                    name = kind
+                    args = [int(a) for a in tok[len(kind):].split("_") if a != ""]
+                    break
+            if name == "SA":
+                store_part(args[0], 0, 4)
+            elif name == "SB":
+                store_part(args[0], 0, 2)
+            elif name == "SC":
+                store_part(args[0], 2, 4)
+            elif name == "EA":
+                evac_part(args[0], 0, 2, False)
+            elif name == "EB":
+                evac_part(args[0], 2, 4, True)
+            elif name == "w":
+                widen(*args)
+            elif name == "I":
+                interleave(*args)
+            elif name == "Q":
+                quantize(*args)
+            elif name == "X":
+                w_transpose(*args)
+            elif name == "WE":
+                w_evac(*args)
+            elif name == "QW":
+                w_quantize(*args)
+            elif name == "Ma" and len(args) == 2:
+                sweep_a(*args)
+            elif name == "Mb":
+                sweep_b(*args)
+            elif name == "Ma":
+                recompute(*args)
+            elif name == "BN":
+                bn(*args)
+            elif name == "AG":
+                aggr(*args)
+            elif name == "SQ":
+                root()
+            elif name == "P":
+                param(*args)
+            elif name == "R":
+                raw(*args)
+            elif name == "N":
+                norm(*args)
+            elif name == "L":
+                leaky(*args)
+            elif name == "Ta":
+                turn(args[0], (0,))
+            elif name == "Tb":
+                turn(args[0], (1, 2))
+            elif name == "T":
+                turn(args[0], (3,))
+            elif name == "E":
+                evac(*args)
+            elif name == "ST":
+                store(*args)
+            else:
+                assert False, tok

@@ -22,29 +22,15 @@ NG = 2
 EPS = 1e-5
 SLOPE = 0.01
 
-S_INTERLEAVES = (6, 7)
-V_EVACS = (3, 5, 7, 9, 11, 13, 15)
-ORDER = (
-    "w0_0 w0_2 w0_1 w0_3 w1_0 I0 w1_1 X0_0 X0_1 X0_2 w1_2 X0_3 X0_4 X0_5 "
-    "X0_6 WE0_0 w1_3 X0_7 X1_0 X1_1 Q0 X1_2 X1_3 X1_4 w2_0 X1_5 WE0_1 X1_6 "
-    "X1_7 w2_1 WE1_0 w2_2 WE1_1 w2_3 QW0 w3_0 QW1 Ma0_0 w3_1 I1 Ma0_1 w3_2 "
-    "Ma0_2 Ma0_3 w3_3 I2 w4_0 w4_1 Q1 w4_2 w4_3 Q2 Mb0_0 w5_0 I3 Mb0_1 "
-    "Mb0_2 w5_1 Mb0_3 Ma1_0 w5_2 Ma1_1 BN0_0 Ma1_2 w5_3 Ma1_3 Q3 w6_0 BN0_1 w6_1 "
-    "Mb1_0 BN0_2 Mb1_1 w6_2 Mb1_2 BN0_3 Mb1_3 w6_3 I4 I6 I5 Q4 w7_0 Q5 "
-    "w7_1 Ma2_0 BN1_0 Ma2_1 w7_2 Ma2_2 BN1_1 Ma2_3 w7_3 Mb2_0 BN1_2 Mb2_1 I7 Mb2_2 "
-    "BN1_3 Mb2_3 Q6 BN2_0 Ma3_0 BN2_1 Ma3_1 Ma3_2 R0 Ma3_3 Q7 R1 BN2_2 R2 "
-    "Mb3_0 BN2_3 Mb3_1 R3 Mb3_2 BN3_0 Mb3_3 BN3_1 BN3_2 BN3_3 AG0 AG1 AG2 AG3 "
-    "SQ P0 P1 P2 P3 N0 L0 N4 N1 N5 L1 Ta0 Tb0 N6 "
-    "T0 Ma8 N2 L2 E0 Ta1 Tb1 N3 N7 T1 L3 Ta2 Tb2 T2 "
-    "E1 Ma9 L4 E2 Ta3 L5 ST0 Tb3 N8 T3 L6 Ta4 Tb4 N9 "
-    "T4 Ta5 E3 Tb5 T5 Ma10 E4 E5 ST1 Ma11 L7 N10 Ta6 L8 "
-    "Tb6 N11 T6 ST2 Ta7 Tb7 L9 T7 Ma12 E6 E7 Ma13 L10 N12 "
-    "Ta8 ST3 Tb8 L11 N13 T8 Ta9 Tb9 T9 Ma14 L12 E8 E9 Ma15 "
-    "N14 L13 Ta10 ST4 Tb10 N15 T10 Ta11 Tb11 L14 T11 Ta12 E10 Tb12 "
-    "T12 E11 E12 L15 Ta13 Tb13 T13 ST5 Ta14 Tb14 T14 E13 Ta15 Tb15 "
-    "E14 T15 ST6 SA14 EA15 EB15 SB15 SC15 "
-)
 V_WIDENS = ((0, 2), (0, 3))
+V_EVACS = (2, 4, 8, 10, 12, 14)
+LEAD = 2
+RC1 = 5
+RC2 = 7
+S_INTERLEAVES = (6, 7)
+S_WEVAC = False
+P_INTERLEAVES = ()
+P_NORMS = False
 
 
 def tile_yuyipointupdate_pb_kernel(tc, h1_bytes, h1_scale, W2, g2, b2, out):
@@ -54,8 +40,8 @@ def tile_yuyipointupdate_pb_kernel(tc, h1_bytes, h1_scale, W2, g2, b2, out):
         keep = ctx.enter_context(tc.tile_pool(name="keep", bufs=1))
         grp_pool = ctx.enter_context(tc.tile_pool(name="grp", bufs=4))
         yr_pool = ctx.enter_context(tc.tile_pool(name="yr", bufs=4))
-        o_pool = ctx.enter_context(tc.tile_pool(name="osb", bufs=4))
-        psum = ctx.enter_context(tc.psum_pool(name="psum", bufs=4))
+        o_pool = ctx.enter_context(tc.tile_pool(name="osb", bufs=8))
+        psum = ctx.enter_context(tc.psum_pool(name="psum", bufs=1))
         ctx.enter_context(tc.manual_schedule())
 
         hscale = const.tile([P, NG, 8], F32, name="hscale")
@@ -89,12 +75,13 @@ def tile_yuyipointupdate_pb_kernel(tc, h1_bytes, h1_scale, W2, g2, b2, out):
         one = const.tile([P, 1], F32, name="one")
         nc.vector.memset(one[:], 1.0)
         warm = const.tile([P, 1], F32, name="warm")
-        nc.scalar.activation(out=warm[:], in_=one[:], func=ACT.Sqrt)
+        nc.scalar.activation(out=warm[:], in_=one[:], func=ACT.Abs_reciprocal_sqrt)
         ident = const.tile([P, P], F32, name="ident")
         make_identity(nc, ident[:])
-        g2f = const.tile([P, NOT, 1], F32, name="g2f")
+        g2pm = const.tile([P, NOT, 2], F32, name="g2pm")
         b2f = const.tile([P, NOT, 1], F32, name="b2f")
-        nc.gpsimd.tensor_copy(out=g2f[:], in_=g2raw[:])
+        nc.gpsimd.tensor_copy(out=g2pm[:, :, 0:1], in_=g2raw[:])
+        nc.gpsimd.tensor_scalar(out=g2pm[:, :, 1:2], in0=g2raw[:], scalar1=-1.0, scalar2=0.0, op0=ALU.mult, op1=ALU.add)
         nc.gpsimd.tensor_copy(out=b2f[:], in_=b2raw[:])
 
         planes = []
@@ -113,24 +100,32 @@ def tile_yuyipointupdate_pb_kernel(tc, h1_bytes, h1_scale, W2, g2, b2, out):
             wscl.append(keep.tile([P, 512], U8, name="wscl%d" % g, align_bytes=64))
         stats = const.tile([P, NOT, NB, 6], F32, name="stats")
         mv = const.tile([P, NOT, 2], F32, name="mv")
+        rstd = const.tile([P, NOT, 1], F32, name="rstd")
+        gg = const.tile([P, NOT, 2], F32, name="gg")
+        shift = const.tile([P, NOT, 1], F32, name="shift")
         grp = {}
         xt = {}
         z = {}
-
-        items = [(b, ot) for b in (2, 3, 0, 1) for ot in range(NOT)]
+        zbank = {}
+        zs = {}
         y = {}
         r = {}
         pt = {}
+        ptbank = {}
         osb = {}
-        zs = {}
-        sd = const.tile([P, NOT, 1], F32, name="sd")
-        rstd = const.tile([P, NOT, 1], F32, name="rstd")
-        gain = const.tile([P, NOT, 1], F32, name="gain")
-        nmg = const.tile([P, NOT, 1], F32, name="nmg")
-        shift = const.tile([P, NOT, 1], F32, name="shift")
+        freed = []
+        taken = [0]
 
-        def bank(name, tag):
-            return psum.tile([P, NN], F32, name=name, tag=tag, bufs={"A": 3, "B": 1, "Z": 4}[tag])
+        items = [(b, 2 * h + e) for h in range(2) for b in (3, 2, 0, 1) for e in range(2)]
+        bn_order = [(b, ot) for b in range(3) for ot in range(NOT)]
+
+        def bank(k, name):
+            return psum.tile([P, NN], F32, name=name, tag="bank%d" % k)
+
+        def take():
+            k = freed[taken[0]]
+            taken[0] += 1
+            return k
 
         def widen(c, t):
             g = c % 2
@@ -143,33 +138,37 @@ def tile_yuyipointupdate_pb_kernel(tc, h1_bytes, h1_scale, W2, g2, b2, out):
                 nc.scalar.activation(out=dst, in_=src, func=ACT.Copy, scale=sc)
 
         def interleave(c):
-            grp[c] = grp_pool.tile([P, 4 * NN], BF16, name="grp%d" % c, tag="grp", align_bytes=64)
+            grp[c] = grp_pool.tile([P, 4 * NN], BF16, name="grp%d" % c, tag="grp%d" % c, bufs=1, align_bytes=64)
             dst = grp[c][:].rearrange("p (n t) -> p n t", t=4)
             src = planes[c][:].rearrange("p t n -> p n t")
             if c in S_INTERLEAVES:
                 nc.scalar.copy(out=dst, in_=src)
+            elif c in P_INTERLEAVES:
+                nc.gpsimd.tensor_scalar(out=dst, in0=src, scalar1=1.0, scalar2=0.0, op0=ALU.mult, op1=ALU.add)
             else:
                 nc.vector.tensor_copy(out=dst, in_=src)
 
         def quantize(c):
             nc.vector.quantize_mx(out=hcod[c][:].bitcast(FP8X4), scales=hscl[c][:], in_=grp[c][:])
 
-        def w_transpose(h, k):
-            g, u, otl = k // 4, (k % 4) // 2, k % 2
-            if k % 4 == 0:
-                xt[(h, g)] = bank("xt%d%d" % (h, g), "Z")
-            words = wraw[2 * h + otl][:].bitcast(F32)
-            nc.tensor.transpose(
-                xt[(h, g)][:, u * 256 + otl * P:u * 256 + (otl + 1) * P],
-                words[:, 256 * g + u:256 * (g + 1):2],
-                ident[:],
-            )
+        def w_transposes(h, g):
+            xt[(h, g)] = bank(4 + 2 * h + g, "xt%d%d" % (h, g))
+            for u in range(2):
+                for otl in range(2):
+                    words = wraw[2 * h + otl][:].bitcast(F32)
+                    nc.tensor.transpose(
+                        xt[(h, g)][:, u * 256 + otl * P:u * 256 + (otl + 1) * P],
+                        words[:, 256 * g + u:256 * (g + 1):2],
+                        ident[:],
+                    )
 
         def w_evac(h, g):
-            nc.vector.tensor_copy(
-                out=wgrp[g][:].bitcast(F32)[:, h * 512:(h + 1) * 512].rearrange("p (r u) -> p r u", u=2),
-                in_=xt[(h, g)][:].rearrange("p (u r) -> p r u", u=2),
-            )
+            dst = wgrp[g][:].bitcast(F32)[:, h * 512:(h + 1) * 512].rearrange("p (r u) -> p r u", u=2)
+            src = xt[(h, g)][:].rearrange("p (u r) -> p r u", u=2)
+            if S_WEVAC:
+                nc.scalar.copy(out=dst, in_=src)
+            else:
+                nc.vector.tensor_copy(out=dst, in_=src)
 
         def w_quantize(g):
             nc.vector.quantize_mx(out=wcod[g][:].bitcast(FP8X4), scales=wscl[g][:], in_=wgrp[g][:])
@@ -187,16 +186,13 @@ def tile_yuyipointupdate_pb_kernel(tc, h1_bytes, h1_scale, W2, g2, b2, out):
                 stop=(g == 1),
             )
 
-        def sweep_a(b, ot):
-            if b % 2 == 1:
-                tag = "Z"
-            else:
-                tag = "A" if ot < 3 else "B"
-            z[(b, ot)] = bank("z%d%d" % (b, ot), tag)
-            mx(z[(b, ot)], ot, 2 * b)
-
-        def sweep_b(b, ot):
-            mx(z[(b, ot)], ot, 2 * b + 1)
+        def sweep(c):
+            b = c // 2
+            for ot in range(NOT):
+                if c % 2 == 0:
+                    zbank[(b, ot)] = 4 * (b % 2) + ot
+                    z[(b, ot)] = bank(zbank[(b, ot)], "z%d%d" % (b, ot))
+                mx(z[(b, ot)], ot, c)
 
         def bn(b, ot):
             nc.vector.bn_stats(out=stats[:, ot, b, :], in_=z[(b, ot)][:])
@@ -204,141 +200,180 @@ def tile_yuyipointupdate_pb_kernel(tc, h1_bytes, h1_scale, W2, g2, b2, out):
         def aggr(ot):
             nc.vector.bn_aggr(out=mv[:, ot, :], in_=stats[:, ot, :, :].rearrange("p b s -> p (b s)"))
 
-        def root():
-            nc.scalar.activation(out=sd[:], in_=mv[:, :, 1:2], func=ACT.Sqrt, bias=EPS, scale=1.0)
+        def par_a(ot):
+            nc.scalar.activation(out=rstd[:, ot, :], in_=mv[:, ot, 1:2], func=ACT.Abs_reciprocal_sqrt, bias=EPS, scale=1.0)
 
-        def param(k):
-            if k == 0:
-                nc.vector.reciprocal(out=rstd[:], in_=sd[:])
-            elif k == 1:
-                nc.vector.tensor_tensor(out=gain[:], in0=g2f[:], in1=rstd[:], op=ALU.mult)
-            elif k == 2:
-                nc.vector.scalar_tensor_tensor(out=nmg[:], in0=mv[:, :, 0:1], scalar=-1.0, in1=gain[:], op0=ALU.mult, op1=ALU.mult)
-            else:
-                nc.vector.tensor_tensor(out=shift[:], in0=nmg[:], in1=b2f[:], op=ALU.add)
+        def par_b(ot):
+            nc.scalar.activation(out=gg[:, ot, :], in_=g2pm[:, ot, :], func=ACT.Copy, scale=rstd[:, ot, :])
 
-        def raw(i):
-            zs[i] = keep.tile([P, NN], F32, name="zs%d" % i)
-            nc.scalar.copy(out=zs[i][:], in_=z[items[i]][:])
+        def par_c(ot):
+            nc.scalar.activation(out=shift[:, ot, :], in_=mv[:, ot, 0:1], func=ACT.Identity, bias=b2f[:, ot, :], scale=gg[:, ot, 1:2])
 
-        def recompute(i):
-            b, ot = items[i]
-            z[(b, ot)] = bank("zz%d%d" % (b, ot), "B" if i in (8, 13) else "Z")
+        def raw(ot):
+            zs[ot] = keep.tile([P, NN], F32, name="zs%d" % ot)
+            nc.scalar.copy(out=zs[ot][:], in_=z[(2, ot)][:])
+            freed.append(zbank[(2, ot)])
+
+        def recompute(b, ot):
+            zbank[(b, ot)] = take()
+            z[(b, ot)] = bank(zbank[(b, ot)], "zz%d%d" % (b, ot))
             mx(z[(b, ot)], ot, 2 * b)
             mx(z[(b, ot)], ot, 2 * b + 1)
 
         def norm(i):
+            if i in y:
+                return
             b, ot = items[i]
-            y[i] = yr_pool.tile([P, NN], F32, name="y%d" % i, tag="y", bufs=8)
-            if i < 4:
-                nc.vector.tensor_scalar(out=y[i][:], in0=zs[i][:], scalar1=gain[:, ot, :], scalar2=shift[:, ot, :], op0=ALU.mult, op1=ALU.add)
+            y[i] = yr_pool.tile([P, NN], F32, name="y%d" % i, tag="y", bufs=16)
+            if b == 2 and P_NORMS:
+                nc.gpsimd.tensor_scalar(out=y[i][:], in0=zs[ot][:], scalar1=gg[:, ot, 0:1], scalar2=shift[:, ot, :], op0=ALU.mult, op1=ALU.add)
+            elif b == 2:
+                nc.vector.tensor_scalar(out=y[i][:], in0=zs[ot][:], scalar1=gg[:, ot, 0:1], scalar2=shift[:, ot, :], op0=ALU.mult, op1=ALU.add)
             else:
-                nc.scalar.activation(out=y[i][:], in_=z[(b, ot)][:], func=ACT.Identity, bias=shift[:, ot, :], scale=gain[:, ot, :])
+                nc.scalar.activation(out=y[i][:], in_=z[(b, ot)][:], func=ACT.Identity, bias=shift[:, ot, :], scale=gg[:, ot, 0:1])
+                freed.append(zbank[(b, ot)])
 
         def leaky(i):
-            r[i] = yr_pool.tile([P, NN], F32, name="r%d" % i, tag="r", bufs=6)
+            r[i] = yr_pool.tile([P, NN], F32, name="r%d" % i, tag="r", bufs=8)
             nc.vector.scalar_tensor_tensor(out=r[i][:], in0=y[i][:], scalar=SLOPE, in1=y[i][:], op0=ALU.mult, op1=ALU.max)
 
-        def turn(i, js):
-            if 0 in js:
-                pt[i] = bank("pt%d" % i, "A")
-            for j in js:
+        def turn(i):
+            ptbank[i] = take()
+            pt[i] = bank(ptbank[i], "pt%d" % i)
+            for j in range(4):
                 nc.tensor.transpose(pt[i][:, j * P:(j + 1) * P], r[i][:, j * P:(j + 1) * P], ident[:])
 
         def evac(i):
-            k, otl = i // 2, i % 2
+            b, ot = items[i]
+            k = (b, ot // 2)
             if k not in osb:
-                osb[k] = o_pool.tile([P, 4, 256], F32, name="osb%d" % k, tag="osb")
-            dst = osb[k][:, :, otl * P:(otl + 1) * P]
+                osb[k] = o_pool.tile([P, 4, 256], F32, name="osb%d%d" % k, tag="osb")
+            dst = osb[k][:, :, (ot % 2) * P:(ot % 2 + 1) * P]
             src = pt[i][:].rearrange("p (j o) -> p j o", j=4)
             if i in V_EVACS:
                 nc.vector.tensor_copy(out=dst, in_=src)
             else:
                 nc.scalar.copy(out=dst, in_=src)
+            freed.append(ptbank[i])
 
-        def evac_part(i, j0, j1, on_vector):
-            k, otl = i // 2, i % 2
-            dst = osb[k][:, j0:j1, otl * P:(otl + 1) * P]
-            src = pt[i][:, j0 * P:j1 * P].rearrange("p (j o) -> p j o", j=j1 - j0)
+        def evac_half(i, half, on_vector):
+            b, ot = items[i]
+            dst = osb[(b, ot // 2)][:, 2 * half:2 * half + 2, (ot % 2) * P:(ot % 2 + 1) * P]
+            src = pt[i][:, 2 * half * P:(2 * half + 2) * P].rearrange("p (j o) -> p j o", j=2)
             if on_vector:
                 nc.vector.tensor_copy(out=dst, in_=src)
             else:
                 nc.scalar.copy(out=dst, in_=src)
+            nc.sync.dma_start(
+                out=out[b].rearrange("(j p) o -> p j o", p=P)[:, 2 * half:2 * half + 2, ot * P:(ot + 1) * P],
+                in_=dst,
+            )
 
-        def store_part(i, j0, j1):
-            k, otl = i // 2, i % 2
+        def store(b, h):
+            nc.sync.dma_start(
+                out=out[b].rearrange("(j p) o -> p j o", p=P)[:, :, h * 256:(h + 1) * 256],
+                in_=osb[(b, h)][:],
+            )
+
+        def store_item(i):
             b, ot = items[i]
             nc.sync.dma_start(
-                out=out[b].rearrange("(j p) o -> p j o", p=P)[:, j0:j1, ot * P:(ot + 1) * P],
-                in_=osb[k][:, j0:j1, otl * P:(otl + 1) * P],
+                out=out[b].rearrange("(j p) o -> p j o", p=P)[:, :, ot * P:(ot + 1) * P],
+                in_=osb[(b, ot // 2)][:, :, (ot % 2) * P:(ot % 2 + 1) * P],
             )
 
-        def store(k):
-            b, ot = items[2 * k]
-            nc.sync.dma_start(
-                out=out[b].rearrange("(j p) o -> p j o", p=P)[:, :, ot * P:(ot + 2) * P],
-                in_=osb[k][:],
-            )
+        for t in range(4):
+            widen(0, t)
+        for t in range(4):
+            widen(1, t)
+        for h in range(2):
+            for g in range(NG):
+                w_transposes(h, g)
+        interleave(0)
+        for g in range(NG):
+            for h in range(2):
+                w_evac(h, g)
+        for c in range(2, 8):
+            for t in range(4):
+                widen(c, t)
+            if c in S_INTERLEAVES or c in P_INTERLEAVES:
+                interleave(c)
 
-        for tok in ORDER.split():
-            name = tok
-            args = []
-            for kind in ("SA", "SB", "SC", "EA", "EB", "Ma", "Mb", "BN", "WE", "QW", "AG", "SQ", "ST", "Ta", "Tb", "w", "I", "Q", "X", "P", "R", "N", "L", "T", "E"):
-                if tok.startswith(kind):
-                    name = kind
-                    args = [int(a) for a in tok[len(kind):].split("_") if a != ""]
-                    break
-            if name == "SA":
-                store_part(args[0], 0, 4)
-            elif name == "SB":
-                store_part(args[0], 0, 2)
-            elif name == "SC":
-                store_part(args[0], 2, 4)
-            elif name == "EA":
-                evac_part(args[0], 0, 2, False)
-            elif name == "EB":
-                evac_part(args[0], 2, 4, True)
-            elif name == "w":
-                widen(*args)
-            elif name == "I":
-                interleave(*args)
-            elif name == "Q":
-                quantize(*args)
-            elif name == "X":
-                w_transpose(*args)
-            elif name == "WE":
-                w_evac(*args)
-            elif name == "QW":
-                w_quantize(*args)
-            elif name == "Ma" and len(args) == 2:
-                sweep_a(*args)
-            elif name == "Mb":
-                sweep_b(*args)
-            elif name == "Ma":
-                recompute(*args)
-            elif name == "BN":
-                bn(*args)
-            elif name == "AG":
-                aggr(*args)
-            elif name == "SQ":
-                root()
-            elif name == "P":
-                param(*args)
-            elif name == "R":
-                raw(*args)
-            elif name == "N":
-                norm(*args)
-            elif name == "L":
-                leaky(*args)
-            elif name == "Ta":
-                turn(args[0], (0,))
-            elif name == "Tb":
-                turn(args[0], (1, 2))
-            elif name == "T":
-                turn(args[0], (3,))
-            elif name == "E":
-                evac(*args)
-            elif name == "ST":
-                store(*args)
-            else:
-                assert False, tok
+        quantize(0)
+        w_quantize(0)
+        sweep(0)
+        interleave(1)
+        w_quantize(1)
+        quantize(1)
+        sweep(1)
+        for c in range(2, 8):
+            if c not in S_INTERLEAVES and c not in P_INTERLEAVES:
+                interleave(c)
+            if c >= 3:
+                bn(*bn_order[2 * (c - 3)])
+                bn(*bn_order[2 * (c - 3) + 1])
+            quantize(c)
+            sweep(c)
+        def nrm(b, ot):
+            norm(items.index((b, ot)))
+
+        raw(0)
+        raw(1)
+        recompute(0, 0)
+        recompute(0, 1)
+        bn(2, 2)
+        bn(3, 0)
+        bn(3, 1)
+        aggr(0)
+        aggr(1)
+        bn(2, 3)
+        bn(3, 2)
+        bn(3, 3)
+        aggr(2)
+        aggr(3)
+        par_a(0)
+        raw(2)
+        par_b(0)
+        par_a(1)
+        raw(3)
+        par_c(0)
+        par_b(1)
+        recompute(1, 0)
+        recompute(1, 1)
+        norm(0)
+        par_c(1)
+        norm(4)
+        norm(1)
+        norm(2)
+
+        chain = [(par_a, 2), (par_b, 2), (par_a, 3), (par_c, 2), (par_b, 3), (par_c, 3)]
+        for rr in range(16 + 2):
+            ahead = rr + LEAD
+            e = rr - 2
+            if 0 <= e < 15 and e not in V_EVACS:
+                evac(e)
+            if ahead < 16 and ahead != 4:
+                norm(ahead)
+            if rr < len(chain):
+                chain[rr][0](chain[rr][1])
+            if rr < 16:
+                leaky(rr)
+            if 0 <= e < 15 and e in V_EVACS:
+                evac(e)
+            if e == 15:
+                evac_half(15, 0, False)
+                evac_half(15, 1, True)
+            if 0 <= e < 15:
+                b, ot = items[e]
+                if e >= 14:
+                    store_item(e)
+                elif ot % 2 == 1:
+                    store(b, ot // 2)
+            if 0 <= rr - 1 < 16:
+                turn(rr - 1)
+            if rr == RC1:
+                recompute(0, 2)
+                recompute(0, 3)
+            if rr == RC2:
+                recompute(1, 2)
+                recompute(1, 3)

@@ -22,13 +22,13 @@ NG = 2
 EPS = 1e-5
 SLOPE = 0.01
 
-V_WIDENS = ((0, 2), (0, 3))
+V_WIDENS = ((0, 2), (0, 3), (1, 2), (1, 3), (2, 2), (2, 3))
 V_EVACS = (2, 4, 8, 10, 12, 14)
 LEAD = 2
 RC1 = 5
 RC2 = 7
-S_INTERLEAVES = (6, 7)
-S_WEVAC = False
+S_INTERLEAVES = (7,)
+S_WEVAC = True
 P_INTERLEAVES = ()
 P_NORMS = False
 
@@ -290,21 +290,21 @@ def tile_yuyipointupdate_pb_kernel(tc, h1_bytes, h1_scale, W2, g2, b2, out):
             for g in range(NG):
                 w_transposes(h, g)
         interleave(0)
-        for g in range(NG):
-            for h in range(2):
+        interleave(1)
+        for h in range(2):
+            for g in range(NG):
                 w_evac(h, g)
+        quantize(0)
         for c in range(2, 8):
             for t in range(4):
                 widen(c, t)
             if c in S_INTERLEAVES or c in P_INTERLEAVES:
                 interleave(c)
 
-        quantize(0)
+        quantize(1)
         w_quantize(0)
         sweep(0)
-        interleave(1)
         w_quantize(1)
-        quantize(1)
         sweep(1)
         for c in range(2, 8):
             if c not in S_INTERLEAVES and c not in P_INTERLEAVES:

@@ -27,6 +27,8 @@ V_EVACS = (2, 4, 8, 10, 12, 14)
 LEAD = 2
 RC1 = 5
 RC2 = 7
+P_SHARES = (4, 5, 6)
+PN = 128
 S_INTERLEAVES = (7,)
 S_WEVAC = True
 P_INTERLEAVES = ()
@@ -137,14 +139,25 @@ def tile_yuyipointupdate_pb_kernel(tc, h1_bytes, h1_scale, W2, g2, b2, out):
             else:
                 nc.scalar.activation(out=dst, in_=src, func=ACT.Copy, scale=sc)
 
+        def new_grp(c):
+            grp[c] = grp_pool.tile([P, 4 * NN], BF16, name="grp%d" % c, tag="grpS" if c in S_INTERLEAVES else "grp", bufs=1 if c in S_INTERLEAVES else 2, align_bytes=64)
+
+        def interleave_pool(c):
+            new_grp(c)
+            nc.gpsimd.tensor_scalar(
+                out=grp[c][:, 0:4 * PN].rearrange("p (n t) -> p n t", t=4),
+                in0=planes[c][:, :, 0:PN].rearrange("p t n -> p n t"),
+                scalar1=1.0, scalar2=0.0, op0=ALU.mult, op1=ALU.add,
+            )
+
         def interleave(c):
-            grp[c] = grp_pool.tile([P, 4 * NN], BF16, name="grp%d" % c, tag="grp%d" % c, bufs=1, align_bytes=64)
-            dst = grp[c][:].rearrange("p (n t) -> p n t", t=4)
-            src = planes[c][:].rearrange("p t n -> p n t")
+            n0 = PN if c in P_SHARES else 0
+            if c not in P_SHARES:
+                new_grp(c)
+            dst = grp[c][:, 4 * n0:].rearrange("p (n t) -> p n t", t=4)
+            src = planes[c][:, :, n0:].rearrange("p t n -> p n t")
             if c in S_INTERLEAVES:
                 nc.scalar.copy(out=dst, in_=src)
-            elif c in P_INTERLEAVES:
-                nc.gpsimd.tensor_scalar(out=dst, in0=src, scalar1=1.0, scalar2=0.0, op0=ALU.mult, op1=ALU.add)
             else:
                 nc.vector.tensor_copy(out=dst, in_=src)
 
@@ -298,22 +311,23 @@ def tile_yuyipointupdate_pb_kernel(tc, h1_bytes, h1_scale, W2, g2, b2, out):
         for c in range(2, 8):
             for t in range(4):
                 widen(c, t)
-            if c in S_INTERLEAVES or c in P_INTERLEAVES:
+            if c in S_INTERLEAVES:
                 interleave(c)
-
-        quantize(1)
         w_quantize(0)
         sweep(0)
         w_quantize(1)
-        sweep(1)
         for c in range(2, 8):
-            if c not in S_INTERLEAVES and c not in P_INTERLEAVES:
+            if c not in S_INTERLEAVES:
                 interleave(c)
+            quantize(c - 1)
+            sweep(c - 1)
+            if c + 1 in P_SHARES:
+                interleave_pool(c + 1)
             if c >= 3:
                 bn(*bn_order[2 * (c - 3)])
                 bn(*bn_order[2 * (c - 3) + 1])
-            quantize(c)
-            sweep(c)
+        quantize(7)
+        sweep(7)
         def nrm(b, ot):
             norm(items.index((b, ot)))
 

@@ -154,11 +154,13 @@ def tile_yuyipointupdate_pb_kernel(tc, h1_bytes, h1_scale, W2, g2, b2, out):
             n0 = PN if c in P_SHARES else 0
             if c not in P_SHARES:
                 new_grp(c)
-            dst = grp[c][:, 4 * n0:].rearrange("p (n t) -> p n t", t=4)
-            src = planes[c][:, :, n0:].rearrange("p t n -> p n t")
             if c in S_INTERLEAVES:
+                dst = grp[c][:, 4 * n0:].rearrange("p (n t) -> p n t", t=4)
+                src = planes[c][:, :, n0:].rearrange("p t n -> p n t")
                 nc.scalar.copy(out=dst, in_=src)
             else:
+                dst = grp[c][:, 4 * n0:].rearrange("p (c i t) -> p c t i", i=4, t=4)
+                src = planes[c][:, :, n0:].rearrange("p t (c i) -> p c t i", i=4)
                 nc.vector.tensor_copy(out=dst, in_=src)
 
         def quantize(c):

@@ -24,9 +24,10 @@ SLOPE = 0.01
 
 V_WIDENS = ((0, 2), (0, 3), (1, 2), (1, 3), (2, 2), (2, 3))
 V_EVACS = (2, 4, 8, 10, 12, 14)
-LEAD = 2
+LEAD = 3
 RC1 = 5
 RC2 = 7
+ELAG = 3
 P_SHARES = (4, 5, 6)
 PN = 128
 S_INTERLEAVES = (7,)
@@ -363,9 +364,9 @@ def tile_yuyipointupdate_pb_kernel(tc, h1_bytes, h1_scale, W2, g2, b2, out):
         norm(2)
 
         chain = [(par_a, 2), (par_b, 2), (par_a, 3), (par_c, 2), (par_b, 3), (par_c, 3)]
-        for rr in range(16 + 2):
+        for rr in range(16 + ELAG):
             ahead = rr + LEAD
-            e = rr - 2
+            e = rr - ELAG
             if 0 <= e < 15 and e not in V_EVACS:
                 evac(e)
             if ahead < 16 and ahead != 4:

@@ -31,9 +31,7 @@ ELAG = 3
 P_SHARES = (4, 5, 6)
 PN = 128
 S_INTERLEAVES = (7,)
-S_WEVAC = True
-P_INTERLEAVES = ()
-P_NORMS = False
+SQ = (2, 3)
 
 
 def tile_yuyipointupdate_pb_kernel(tc, h1_bytes, h1_scale, W2, g2, b2, out):
@@ -101,7 +99,12 @@ def tile_yuyipointupdate_pb_kernel(tc, h1_bytes, h1_scale, W2, g2, b2, out):
             wgrp.append(keep.tile([P, 2048], BF16, name="wgrp%d" % g, align_bytes=64))
             wcod.append(keep.tile([P, 512], U32, name="wcod%d" % g, align_bytes=64))
             wscl.append(keep.tile([P, 512], U8, name="wscl%d" % g, align_bytes=64))
-        stats = const.tile([P, NOT, NB, 6], F32, name="stats")
+        stats = const.tile([P, NOT, 32], F32, name="stats")
+        sums = const.tile([P, NOT, 1], F32, name="sums")
+        sqs = const.tile([P, NOT, 1], F32, name="sqs")
+        m2 = const.tile([P, NOT, 1], F32, name="m2")
+        junk = const.tile([P, NN], F32, name="junk")
+        nc.gpsimd.memset(stats[:, :, 5:6], float(NN))
         mv = const.tile([P, NOT, 2], F32, name="mv")
         rstd = const.tile([P, NOT, 1], F32, name="rstd")
         gg = const.tile([P, NOT, 2], F32, name="gg")
@@ -181,10 +184,7 @@ def tile_yuyipointupdate_pb_kernel(tc, h1_bytes, h1_scale, W2, g2, b2, out):
         def w_evac(h, g):
             dst = wgrp[g][:].bitcast(F32)[:, h * 512:(h + 1) * 512].rearrange("p (r u) -> p r u", u=2)
             src = xt[(h, g)][:].rearrange("p (u r) -> p r u", u=2)
-            if S_WEVAC:
-                nc.scalar.copy(out=dst, in_=src)
-            else:
-                nc.vector.tensor_copy(out=dst, in_=src)
+            nc.scalar.copy(out=dst, in_=src)
 
         def w_quantize(g):
             nc.vector.quantize_mx(out=wcod[g][:].bitcast(FP8X4), scales=wscl[g][:], in_=wgrp[g][:])
@@ -211,10 +211,11 @@ def tile_yuyipointupdate_pb_kernel(tc, h1_bytes, h1_scale, W2, g2, b2, out):
                 mx(z[(b, ot)], ot, c)
 
         def bn(b, ot):
-            nc.vector.bn_stats(out=stats[:, ot, b, :], in_=z[(b, ot)][:])
+            col = {0: 8, 1: 14, 3: 20, 2: 26}[b]
+            nc.vector.bn_stats(out=stats[:, ot, col:col + 6], in_=z[(b, ot)][:])
 
         def aggr(ot):
-            nc.vector.bn_aggr(out=mv[:, ot, :], in_=stats[:, ot, :, :].rearrange("p b s -> p (b s)"))
+            nc.vector.bn_aggr(out=mv[:, ot, :], in_=stats[:, ot, 5:26] if ot in SQ else stats[:, ot, 8:32])
 
         def par_a(ot):
             nc.scalar.activation(out=rstd[:, ot, :], in_=mv[:, ot, 1:2], func=ACT.Abs_reciprocal_sqrt, bias=EPS, scale=1.0)
@@ -227,7 +228,21 @@ def tile_yuyipointupdate_pb_kernel(tc, h1_bytes, h1_scale, W2, g2, b2, out):
 
         def raw(ot):
             zs[ot] = keep.tile([P, NN], F32, name="zs%d" % ot)
-            nc.scalar.copy(out=zs[ot][:], in_=z[(2, ot)][:])
+            if ot in SQ:
+                nc.scalar.activation(out=zs[ot][:], in_=z[(2, ot)][:], func=ACT.Copy, accum_out=sums[:, ot, :])
+            else:
+                nc.scalar.copy(out=zs[ot][:], in_=z[(2, ot)][:])
+
+        def square(ot):
+            nc.scalar.activation(out=junk[:], in_=z[(2, ot)][:], func=ACT.Square, accum_out=sqs[:, ot, :])
+
+        def triple(h):
+            ots = slice(2 * h, 2 * h + 2)
+            nc.gpsimd.tensor_scalar(out=stats[:, ots, 6:7], in0=sums[:, ots, :], scalar1=1.0 / NN, scalar2=0.0, op0=ALU.mult, op1=ALU.add)
+            nc.gpsimd.tensor_tensor(out=m2[:, ots, :], in0=sums[:, ots, :], in1=stats[:, ots, 6:7], op=ALU.mult)
+            nc.gpsimd.tensor_tensor(out=stats[:, ots, 7:8], in0=sqs[:, ots, :], in1=m2[:, ots, :], op=ALU.subtract)
+
+        def free_z2(ot):
             freed.append(zbank[(2, ot)])
 
         def recompute(b, ot):
@@ -241,9 +256,7 @@ def tile_yuyipointupdate_pb_kernel(tc, h1_bytes, h1_scale, W2, g2, b2, out):
                 return
             b, ot = items[i]
             y[i] = yr_pool.tile([P, NN], F32, name="y%d" % i, tag="y", bufs=16)
-            if b == 2 and P_NORMS:
-                nc.gpsimd.tensor_scalar(out=y[i][:], in0=zs[ot][:], scalar1=gg[:, ot, 0:1], scalar2=shift[:, ot, :], op0=ALU.mult, op1=ALU.add)
-            elif b == 2:
+            if b == 2:
                 nc.vector.tensor_scalar(out=y[i][:], in0=zs[ot][:], scalar1=gg[:, ot, 0:1], scalar2=shift[:, ot, :], op0=ALU.mult, op1=ALU.add)
             else:
                 nc.scalar.activation(out=y[i][:], in_=z[(b, ot)][:], func=ACT.Identity, bias=shift[:, ot, :], scale=gg[:, ot, 0:1])
@@ -326,39 +339,51 @@ def tile_yuyipointupdate_pb_kernel(tc, h1_bytes, h1_scale, W2, g2, b2, out):
             sweep(c - 1)
             if c + 1 in P_SHARES:
                 interleave_pool(c + 1)
-            if c >= 3:
+            if 3 <= c < 7:
                 bn(*bn_order[2 * (c - 3)])
                 bn(*bn_order[2 * (c - 3) + 1])
+        tail = [(2, ot) for ot in (0, 1) if ot not in SQ]
+        if tail:
+            bn(*tail[0])
         quantize(7)
         sweep(7)
-        def nrm(b, ot):
-            norm(items.index((b, ot)))
+        if len(tail) > 1:
+            bn(*tail[1])
 
-        raw(0)
-        raw(1)
-        recompute(0, 0)
-        recompute(0, 1)
-        bn(2, 2)
+        for ot in range(NOT):
+            raw(ot)
+            if ot in SQ:
+                square(ot)
+            if ot in SQ or ot < 2:
+                free_z2(ot)
+            if ot == 1:
+                if 0 in SQ:
+                    triple(0)
+                recompute(0, 0)
+                recompute(0, 1)
+        if 2 in SQ:
+            triple(1)
+            recompute(1, 0)
+            recompute(1, 1)
         bn(3, 0)
         bn(3, 1)
         aggr(0)
         aggr(1)
-        bn(2, 3)
+        for ot in (2, 3):
+            if ot not in SQ:
+                bn(2, ot)
+                free_z2(ot)
         bn(3, 2)
         bn(3, 3)
         aggr(2)
         aggr(3)
-        par_a(0)
-        raw(2)
-        par_b(0)
-        par_a(1)
-        raw(3)
-        par_c(0)
-        par_b(1)
-        recompute(1, 0)
-        recompute(1, 1)
+        if 2 not in SQ:
+            recompute(1, 0)
+            recompute(1, 1)
+        for par in (par_a, par_b, par_c):
+            par(0)
+            par(1)
         norm(0)
-        par_c(1)
         norm(4)
         norm(1)
         norm(2)

@@ -22,16 +22,25 @@ NG = 2
 EPS = 1e-5
 SLOPE = 0.01
 
-V_WIDENS = ((0, 2), (0, 3), (1, 2), (1, 3), (2, 2), (2, 3))
-V_EVACS = (2, 4, 8, 10, 12, 14)
-LEAD = 3
-RC1 = 5
-RC2 = 7
-ELAG = 3
+V_WIDENS = ((0, 1), (0, 2), (0, 3), (1, 3), (2, 2), (2, 3))
+L1 = 5
+L2 = 2
+L3 = 1
+RC1 = 3
+RC2 = 6
+SQ = (2, 3)
+VN = (3,)
+CHAIN = {3: ((0, 2), (1, 2), (0, 3), (1, 3)), 4: ((2, 2), (3, 2), (2, 3), (3, 3))}
+V_NORMS = ()
+G_LEAKY = ()
+V_SMALLS = (0, 1, 2, 3, 7)
+SINGLE = ((1, 1),)
 P_SHARES = (4, 5, 6)
 PN = 128
 S_INTERLEAVES = (7,)
-SQ = (2, 3)
+S_WEVAC = True
+P_INTERLEAVES = ()
+P_NORMS = False
 
 
 def tile_yuyipointupdate_pb_kernel(tc, h1_bytes, h1_scale, W2, g2, b2, out):
@@ -61,7 +70,9 @@ def tile_yuyipointupdate_pb_kernel(tc, h1_bytes, h1_scale, W2, g2, b2, out):
             b, g = c // 2, c % 2
             nc.sync.dma_start(out=hb[c][:], in_=h1_bytes[b].rearrange("(g p t) n -> g p t n", p=P, t=4)[g])
 
-        load_h(0)
+        for half in range(2):
+            ts = slice(2 * half, 2 * half + 2)
+            nc.sync.dma_start(out=hb[0][:, ts, :], in_=h1_bytes[0].rearrange("(g p t) n -> g p t n", p=P, t=4)[0][:, ts, :])
         load_h(1)
         for ot in range(NOT):
             nc.sync.dma_start(out=wraw[ot][:], in_=W2[ot * P:(ot + 1) * P, :])
@@ -107,7 +118,8 @@ def tile_yuyipointupdate_pb_kernel(tc, h1_bytes, h1_scale, W2, g2, b2, out):
         nc.gpsimd.memset(stats[:, :, 5:6], float(NN))
         mv = const.tile([P, NOT, 2], F32, name="mv")
         rstd = const.tile([P, NOT, 1], F32, name="rstd")
-        gg = const.tile([P, NOT, 2], F32, name="gg")
+        gg = const.tile([P, NOT, 1], F32, name="gg")
+        mg = const.tile([P, NOT, 1], F32, name="mg")
         shift = const.tile([P, NOT, 1], F32, name="shift")
         grp = {}
         xt = {}
@@ -121,8 +133,9 @@ def tile_yuyipointupdate_pb_kernel(tc, h1_bytes, h1_scale, W2, g2, b2, out):
         osb = {}
         freed = []
         taken = [0]
+        gt = {}
+        sm = {}
 
-        items = [(b, 2 * h + e) for h in range(2) for b in (3, 2, 0, 1) for e in range(2)]
         bn_order = [(b, ot) for b in range(3) for ot in range(NOT)]
 
         def bank(k, name):
@@ -184,7 +197,10 @@ def tile_yuyipointupdate_pb_kernel(tc, h1_bytes, h1_scale, W2, g2, b2, out):
         def w_evac(h, g):
             dst = wgrp[g][:].bitcast(F32)[:, h * 512:(h + 1) * 512].rearrange("p (r u) -> p r u", u=2)
             src = xt[(h, g)][:].rearrange("p (u r) -> p r u", u=2)
-            nc.scalar.copy(out=dst, in_=src)
+            if S_WEVAC:
+                nc.scalar.copy(out=dst, in_=src)
+            else:
+                nc.vector.tensor_copy(out=dst, in_=src)
 
         def w_quantize(g):
             nc.vector.quantize_mx(out=wcod[g][:].bitcast(FP8X4), scales=wscl[g][:], in_=wgrp[g][:])
@@ -220,11 +236,14 @@ def tile_yuyipointupdate_pb_kernel(tc, h1_bytes, h1_scale, W2, g2, b2, out):
         def par_a(ot):
             nc.scalar.activation(out=rstd[:, ot, :], in_=mv[:, ot, 1:2], func=ACT.Abs_reciprocal_sqrt, bias=EPS, scale=1.0)
 
+        def par_m(ot):
+            nc.scalar.activation(out=mg[:, ot, :], in_=mv[:, ot, 0:1], func=ACT.Copy, scale=g2pm[:, ot, 1:2])
+
         def par_b(ot):
-            nc.scalar.activation(out=gg[:, ot, :], in_=g2pm[:, ot, :], func=ACT.Copy, scale=rstd[:, ot, :])
+            nc.scalar.activation(out=gg[:, ot, :], in_=g2pm[:, ot, 0:1], func=ACT.Copy, scale=rstd[:, ot, :])
 
         def par_c(ot):
-            nc.scalar.activation(out=shift[:, ot, :], in_=mv[:, ot, 0:1], func=ACT.Identity, bias=b2f[:, ot, :], scale=gg[:, ot, 1:2])
+            nc.scalar.activation(out=shift[:, ot, :], in_=mg[:, ot, :], func=ACT.Identity, bias=b2f[:, ot, :], scale=rstd[:, ot, :])
 
         def raw(ot):
             zs[ot] = keep.tile([P, NN], F32, name="zs%d" % ot)
@@ -236,8 +255,8 @@ def tile_yuyipointupdate_pb_kernel(tc, h1_bytes, h1_scale, W2, g2, b2, out):
         def square(ot):
             nc.scalar.activation(out=junk[:], in_=z[(2, ot)][:], func=ACT.Square, accum_out=sqs[:, ot, :])
 
-        def triple(h):
-            ots = slice(2 * h, 2 * h + 2)
+        def triple(first, last):
+            ots = slice(first, last + 1)
             nc.gpsimd.tensor_scalar(out=stats[:, ots, 6:7], in0=sums[:, ots, :], scalar1=1.0 / NN, scalar2=0.0, op0=ALU.mult, op1=ALU.add)
             nc.gpsimd.tensor_tensor(out=m2[:, ots, :], in0=sums[:, ots, :], in1=stats[:, ots, 6:7], op=ALU.mult)
             nc.gpsimd.tensor_tensor(out=stats[:, ots, 7:8], in0=sqs[:, ots, :], in1=m2[:, ots, :], op=ALU.subtract)
@@ -251,65 +270,87 @@ def tile_yuyipointupdate_pb_kernel(tc, h1_bytes, h1_scale, W2, g2, b2, out):
             mx(z[(b, ot)], ot, 2 * b)
             mx(z[(b, ot)], ot, 2 * b + 1)
 
-        def norm(i):
-            if i in y:
-                return
-            b, ot = items[i]
-            y[i] = yr_pool.tile([P, NN], F32, name="y%d" % i, tag="y", bufs=16)
+        def norm(b, ot, on_vector=False):
+            y[(b, ot)] = yr_pool.tile([P, NN], F32, name="y%d%d" % (b, ot), tag="yp" if b == 2 else "y", bufs=4 if b == 2 else 8)
             if b == 2:
-                nc.vector.tensor_scalar(out=y[i][:], in0=zs[ot][:], scalar1=gg[:, ot, 0:1], scalar2=shift[:, ot, :], op0=ALU.mult, op1=ALU.add)
+                eng = nc.vector if (b, ot) in V_NORMS else nc.gpsimd
+                eng.tensor_scalar(out=y[(b, ot)][:], in0=zs[ot][:], scalar1=gg[:, ot, 0:1], scalar2=shift[:, ot, :], op0=ALU.mult, op1=ALU.add)
+            elif on_vector:
+                nc.vector.tensor_scalar(out=y[(b, ot)][:], in0=z[(b, ot)][:], scalar1=gg[:, ot, 0:1], scalar2=shift[:, ot, :], op0=ALU.mult, op1=ALU.add)
+                freed.append(zbank[(b, ot)])
             else:
-                nc.scalar.activation(out=y[i][:], in_=z[(b, ot)][:], func=ACT.Identity, bias=shift[:, ot, :], scale=gg[:, ot, 0:1])
+                nc.scalar.activation(out=y[(b, ot)][:], in_=z[(b, ot)][:], func=ACT.Identity, bias=shift[:, ot, :], scale=gg[:, ot, 0:1])
                 freed.append(zbank[(b, ot)])
 
-        def leaky(i):
-            r[i] = yr_pool.tile([P, NN], F32, name="r%d" % i, tag="r", bufs=8)
-            nc.vector.scalar_tensor_tensor(out=r[i][:], in0=y[i][:], scalar=SLOPE, in1=y[i][:], op0=ALU.mult, op1=ALU.max)
+        def gleak_a(ot):
+            gt[ot] = yr_pool.tile([P, NN], F32, name="gt%d" % ot, tag="gt", bufs=2)
+            nc.gpsimd.tensor_scalar(out=gt[ot][:], in0=y[(2, ot)][:], scalar1=0.0, scalar2=SLOPE - 1.0, op0=ALU.min, op1=ALU.mult)
 
-        def turn(i):
-            ptbank[i] = take()
-            pt[i] = bank(ptbank[i], "pt%d" % i)
+        def gleak_b(ot):
+            r[(2, ot)] = yr_pool.tile([P, NN], F32, name="gr%d" % ot, tag="gr", bufs=4)
+            nc.gpsimd.tensor_tensor(out=r[(2, ot)][:], in0=y[(2, ot)][:], in1=gt[ot][:], op=ALU.add)
+
+        def turn(b, ot):
+            it = (b, ot)
+            src = r[it] if it in G_LEAKY else y[it]
+            ptbank[it] = take()
+            pt[it] = bank(ptbank[it], "pt%d%d" % it)
             for j in range(4):
-                nc.tensor.transpose(pt[i][:, j * P:(j + 1) * P], r[i][:, j * P:(j + 1) * P], ident[:])
+                nc.tensor.transpose(pt[it][:, j * P:(j + 1) * P], src[:, j * P:(j + 1) * P], ident[:])
 
-        def evac(i):
-            b, ot = items[i]
+        def osb_of(b, ot):
             k = (b, ot // 2)
             if k not in osb:
                 osb[k] = o_pool.tile([P, 4, 256], F32, name="osb%d%d" % k, tag="osb")
-            dst = osb[k][:, :, (ot % 2) * P:(ot % 2 + 1) * P]
-            src = pt[i][:].rearrange("p (j o) -> p j o", j=4)
-            if i in V_EVACS:
-                nc.vector.tensor_copy(out=dst, in_=src)
-            else:
-                nc.scalar.copy(out=dst, in_=src)
-            freed.append(ptbank[i])
+            return osb[k][:, :, (ot % 2) * P:(ot % 2 + 1) * P]
 
-        def evac_half(i, half, on_vector):
-            b, ot = items[i]
-            dst = osb[(b, ot // 2)][:, 2 * half:2 * half + 2, (ot % 2) * P:(ot % 2 + 1) * P]
-            src = pt[i][:, 2 * half * P:(2 * half + 2) * P].rearrange("p (j o) -> p j o", j=2)
+        def small(b, ot, on_vector):
+            it = (b, ot)
+            sm[it] = yr_pool.tile([P, NN], F32, name="sm%d%d" % it, tag="smV" if on_vector else "sm", bufs=4)
+            if on_vector:
+                nc.vector.tensor_scalar(out=sm[it][:], in0=pt[it][:], scalar1=SLOPE, scalar2=None, op0=ALU.mult)
+            else:
+                nc.scalar.activation(out=sm[it][:], in_=pt[it][:], func=ACT.Copy, scale=SLOPE)
+
+        def larger(b, ot, half=None):
+            it = (b, ot)
+            js = slice(0, 4) if half is None else slice(2 * half, 2 * half + 2)
+            n = slice(js.start * P, js.stop * P)
+            nc.vector.tensor_tensor(
+                out=osb_of(b, ot)[:, js, :],
+                in0=pt[it][:, n].rearrange("p (j o) -> p j o", o=P),
+                in1=sm[it][:, n].rearrange("p (j o) -> p j o", o=P),
+                op=ALU.max,
+            )
+            if half is None or half == 1:
+                freed.append(ptbank[it])
+
+        def evac(b, ot, on_vector):
+            it = (b, ot)
+            dst = osb_of(b, ot)
+            src = pt[it][:].rearrange("p (j o) -> p j o", j=4)
             if on_vector:
                 nc.vector.tensor_copy(out=dst, in_=src)
             else:
                 nc.scalar.copy(out=dst, in_=src)
-            nc.sync.dma_start(
-                out=out[b].rearrange("(j p) o -> p j o", p=P)[:, 2 * half:2 * half + 2, ot * P:(ot + 1) * P],
-                in_=dst,
-            )
+            freed.append(ptbank[it])
 
-        def store(b, h):
-            nc.sync.dma_start(
-                out=out[b].rearrange("(j p) o -> p j o", p=P)[:, :, h * 256:(h + 1) * 256],
-                in_=osb[(b, h)][:],
-            )
+        stored = {}
 
-        def store_item(i):
-            b, ot = items[i]
-            nc.sync.dma_start(
-                out=out[b].rearrange("(j p) o -> p j o", p=P)[:, :, ot * P:(ot + 1) * P],
-                in_=osb[(b, ot // 2)][:, :, (ot % 2) * P:(ot % 2 + 1) * P],
-            )
+        def done(b, ot):
+            k = (b, ot // 2)
+            if k in SINGLE:
+                nc.sync.dma_start(
+                    out=out[b].rearrange("(j p) o -> p j o", p=P)[:, :, ot * P:(ot + 1) * P],
+                    in_=osb[k][:, :, (ot % 2) * P:(ot % 2 + 1) * P],
+                )
+                return
+            stored[k] = stored.get(k, 0) + 1
+            if stored[k] == 2:
+                nc.sync.dma_start(
+                    out=out[b].rearrange("(j p) o -> p j o", p=P)[:, :, (ot // 2) * 256:(ot // 2 + 1) * 256],
+                    in_=osb[k][:],
+                )
 
         for t in range(4):
             widen(0, t)
@@ -343,76 +384,65 @@ def tile_yuyipointupdate_pb_kernel(tc, h1_bytes, h1_scale, W2, g2, b2, out):
                 bn(*bn_order[2 * (c - 3)])
                 bn(*bn_order[2 * (c - 3) + 1])
         tail = [(2, ot) for ot in (0, 1) if ot not in SQ]
-        if tail:
+        if len(tail) > 1:
             bn(*tail[0])
         quantize(7)
         sweep(7)
-        if len(tail) > 1:
-            bn(*tail[1])
+        if tail:
+            bn(*tail[-1])
 
-        for ot in range(NOT):
+        for ot in (2, 3):
+            raw(ot)
+            square(ot)
+            free_z2(ot)
+        triple(2, 3)
+        recompute(0, 0)
+        recompute(0, 1)
+        for ot in (0, 1):
             raw(ot)
             if ot in SQ:
                 square(ot)
-            if ot in SQ or ot < 2:
-                free_z2(ot)
-            if ot == 1:
-                if 0 in SQ:
-                    triple(0)
-                recompute(0, 0)
-                recompute(0, 1)
-        if 2 in SQ:
-            triple(1)
-            recompute(1, 0)
-            recompute(1, 1)
+                triple(ot, ot)
+            free_z2(ot)
+        recompute(1, 0)
+        recompute(1, 1)
         bn(3, 0)
         bn(3, 1)
         aggr(0)
         aggr(1)
-        for ot in (2, 3):
-            if ot not in SQ:
-                bn(2, ot)
-                free_z2(ot)
         bn(3, 2)
         bn(3, 3)
         aggr(2)
         aggr(3)
-        if 2 not in SQ:
-            recompute(1, 0)
-            recompute(1, 1)
-        for par in (par_a, par_b, par_c):
-            par(0)
-            par(1)
-        norm(0)
-        norm(4)
-        norm(1)
-        norm(2)
+        par_a(0)
+        par_m(0)
+        par_a(1)
+        par_m(1)
+        par_b(0)
+        par_c(0)
+        par_b(1)
+        par_c(1)
 
-        chain = [(par_a, 2), (par_b, 2), (par_a, 3), (par_c, 2), (par_b, 3), (par_c, 3)]
-        for rr in range(16 + ELAG):
-            ahead = rr + LEAD
-            e = rr - ELAG
-            if 0 <= e < 15 and e not in V_EVACS:
-                evac(e)
-            if ahead < 16 and ahead != 4:
-                norm(ahead)
-            if rr < len(chain):
-                chain[rr][0](chain[rr][1])
-            if rr < 16:
-                leaky(rr)
-            if 0 <= e < 15 and e in V_EVACS:
-                evac(e)
-            if e == 15:
-                evac_half(15, 0, False)
-                evac_half(15, 1, True)
-            if 0 <= e < 15:
-                b, ot = items[e]
-                if e >= 14:
-                    store_item(e)
-                elif ot % 2 == 1:
-                    store(b, ot // 2)
-            if 0 <= rr - 1 < 16:
-                turn(rr - 1)
+        order = [(b, 2 * h + e) for h in range(2) for b in (3, 0, 2, 1) for e in range(2)]
+        n = len(order)
+        for rr in range(-L1, n + L3):
+            i = rr + L1
+            if 0 <= i < n:
+                if i % 8 == 2:
+                    norm(2, 2 * (i // 8))
+                    norm(2, 2 * (i // 8) + 1)
+                if order[i][0] != 2:
+                    norm(*order[i], on_vector=(i in VN))
+            for par, ot in CHAIN.get(i, ()):
+                (par_a, par_m, par_b, par_c)[par](ot)
+            if 0 <= rr + L2 < n:
+                turn(*order[rr + L2])
+            if 0 <= rr < n:
+                small(*order[rr], rr in V_SMALLS)
+            e = rr - L3
+            if e >= 0:
+                larger(*order[e])
+                done(*order[e])
             if rr == RC1:
                 recompute(0, 2)
                 recompute(0, 3)

@@ -22,7 +22,7 @@ NG = 2
 EPS = 1e-5
 SLOPE = 0.01
 
-V_WIDENS = ((0, 1), (0, 2), (0, 3), (1, 3), (2, 2), (2, 3))
+V_WIDENS = ((0, 1), (0, 2), (0, 3), (1, 3), (2, 2), (2, 3), (3, 3))
 L1 = 5
 L2 = 2
 L3 = 1

@@ -23,18 +23,22 @@ EPS = 1e-5
 SLOPE = 0.01
 
 V_WIDENS = ((0, 1), (0, 2), (0, 3), (1, 3), (2, 2), (2, 3), (3, 3))
-L1 = 5
+L1 = 4
 L2 = 2
 L3 = 1
-RC1 = 3
-RC2 = 6
+RC1 = 2
+RC2 = 5
 SQ = (2, 3)
 VN = (3,)
 CHAIN = {3: ((0, 2), (1, 2), (0, 3), (1, 3)), 4: ((2, 2), (3, 2), (2, 3), (3, 3))}
 V_NORMS = ()
-G_LEAKY = ()
-V_SMALLS = (0, 1, 2, 3, 7)
-SINGLE = ((1, 1),)
+G_LEAKY = ((2, 0), (2, 1))
+VH = ((1, 0), (1, 1))
+EARLY = False
+G2 = 8
+BY_UNIT = ((3, 0), (0, 0), (2, 1), (0, 1), (1, 0), (3, 1), (2, 0), (1, 1))
+PAIRS = ((3, 0), (0, 0), (1, 0), (3, 1), (2, 1), (0, 1), (2, 0), (1, 1))
+V_SMALLS = (0, 1, 3, 6, 9, 12)
 P_SHARES = (4, 5, 6)
 PN = 128
 S_INTERLEAVES = (7,)
@@ -134,6 +138,7 @@ def tile_yuyipointupdate_pb_kernel(tc, h1_bytes, h1_scale, W2, g2, b2, out):
         freed = []
         taken = [0]
         gt = {}
+        gu = {}
         sm = {}
 
         bn_order = [(b, ot) for b in range(3) for ot in range(NOT)]
@@ -270,86 +275,80 @@ def tile_yuyipointupdate_pb_kernel(tc, h1_bytes, h1_scale, W2, g2, b2, out):
             mx(z[(b, ot)], ot, 2 * b)
             mx(z[(b, ot)], ot, 2 * b + 1)
 
-        def norm(b, ot, on_vector=False):
-            y[(b, ot)] = yr_pool.tile([P, NN], F32, name="y%d%d" % (b, ot), tag="yp" if b == 2 else "y", bufs=4 if b == 2 else 8)
+        def norm(b, ot, on_vector=False, halves=(0, 1)):
+            it = (b, ot)
+            if it not in y:
+                y[it] = yr_pool.tile([P, NN], F32, name="y%d%d" % it, tag="yp" if b == 2 else "y", bufs=4 if b == 2 else 8)
+            cols = slice(halves[0] * 256, halves[-1] * 256 + 256)
+            dst = y[it][:, cols]
             if b == 2:
-                eng = nc.vector if (b, ot) in V_NORMS else nc.gpsimd
-                eng.tensor_scalar(out=y[(b, ot)][:], in0=zs[ot][:], scalar1=gg[:, ot, 0:1], scalar2=shift[:, ot, :], op0=ALU.mult, op1=ALU.add)
-            elif on_vector:
-                nc.vector.tensor_scalar(out=y[(b, ot)][:], in0=z[(b, ot)][:], scalar1=gg[:, ot, 0:1], scalar2=shift[:, ot, :], op0=ALU.mult, op1=ALU.add)
-                freed.append(zbank[(b, ot)])
+                nc.gpsimd.tensor_scalar(out=dst, in0=zs[ot][:, cols], scalar1=gg[:, ot, 0:1], scalar2=shift[:, ot, :], op0=ALU.mult, op1=ALU.add)
+                return
+            if on_vector:
+                nc.vector.tensor_scalar(out=dst, in0=z[it][:, cols], scalar1=gg[:, ot, 0:1], scalar2=shift[:, ot, :], op0=ALU.mult, op1=ALU.add)
             else:
-                nc.scalar.activation(out=y[(b, ot)][:], in_=z[(b, ot)][:], func=ACT.Identity, bias=shift[:, ot, :], scale=gg[:, ot, 0:1])
-                freed.append(zbank[(b, ot)])
+                nc.scalar.activation(out=dst, in_=z[it][:, cols], func=ACT.Identity, bias=shift[:, ot, :], scale=gg[:, ot, 0:1])
+            if halves[-1] == 1:
+                freed.append(zbank[it])
 
         def gleak_a(ot):
             gt[ot] = yr_pool.tile([P, NN], F32, name="gt%d" % ot, tag="gt", bufs=2)
-            nc.gpsimd.tensor_scalar(out=gt[ot][:], in0=y[(2, ot)][:], scalar1=0.0, scalar2=SLOPE - 1.0, op0=ALU.min, op1=ALU.mult)
+            nc.gpsimd.tensor_scalar(out=gt[ot][:], in0=y[(2, ot)][:], scalar1=0.0, scalar2=None, op0=ALU.min)
 
         def gleak_b(ot):
-            r[(2, ot)] = yr_pool.tile([P, NN], F32, name="gr%d" % ot, tag="gr", bufs=4)
-            nc.gpsimd.tensor_tensor(out=r[(2, ot)][:], in0=y[(2, ot)][:], in1=gt[ot][:], op=ALU.add)
+            gu[ot] = yr_pool.tile([P, NN], F32, name="gu%d" % ot, tag="gu", bufs=2)
+            nc.gpsimd.tensor_scalar(out=gu[ot][:], in0=gt[ot][:], scalar1=SLOPE - 1.0, scalar2=0.0, op0=ALU.mult, op1=ALU.add)
 
-        def turn(b, ot):
-            it = (b, ot)
-            src = r[it] if it in G_LEAKY else y[it]
-            ptbank[it] = take()
-            pt[it] = bank(ptbank[it], "pt%d%d" % it)
-            for j in range(4):
-                nc.tensor.transpose(pt[it][:, j * P:(j + 1) * P], src[:, j * P:(j + 1) * P], ident[:])
+        def gleak_c(ot):
+            r[(2, ot)] = yr_pool.tile([P, NN], F32, name="gr%d" % ot, tag="gr", bufs=2)
+            nc.gpsimd.tensor_tensor(out=r[(2, ot)][:], in0=y[(2, ot)][:], in1=gu[ot][:], op=ALU.add)
 
-        def osb_of(b, ot):
-            k = (b, ot // 2)
-            if k not in osb:
-                osb[k] = o_pool.tile([P, 4, 256], F32, name="osb%d%d" % k, tag="osb")
-            return osb[k][:, :, (ot % 2) * P:(ot % 2 + 1) * P]
+        def turn(b, h, u):
+            k = (b, h, u)
+            ptbank[k] = take()
+            pt[k] = bank(ptbank[k], "pt%d%d%d" % k)
+            for j in range(2):
+                for e in range(2):
+                    it = (b, 2 * h + e)
+                    src = r[it] if it in G_LEAKY else y[it]
+                    nc.tensor.transpose(
+                        pt[k][:, (2 * j + e) * P:(2 * j + e + 1) * P],
+                        src[:, (2 * u + j) * P:(2 * u + j + 1) * P],
+                        ident[:],
+                    )
 
-        def small(b, ot, on_vector):
-            it = (b, ot)
-            sm[it] = yr_pool.tile([P, NN], F32, name="sm%d%d" % it, tag="smV" if on_vector else "sm", bufs=4)
+        def osb_of(b, h, u):
+            if (b, h) not in osb:
+                osb[(b, h)] = o_pool.tile([P, 4, 256], F32, name="osb%d%d" % (b, h), tag="osb")
+            return osb[(b, h)][:, 2 * u:2 * u + 2, :].rearrange("p j o -> p (j o)")
+
+        def small(b, h, u, on_vector):
+            k = (b, h, u)
+            sm[k] = yr_pool.tile([P, NN], F32, name="sm%d%d%d" % k, tag="smV" if on_vector else "sm", bufs=4)
             if on_vector:
-                nc.vector.tensor_scalar(out=sm[it][:], in0=pt[it][:], scalar1=SLOPE, scalar2=None, op0=ALU.mult)
+                nc.vector.tensor_scalar(out=sm[k][:], in0=pt[k][:], scalar1=SLOPE, scalar2=None, op0=ALU.mult)
             else:
-                nc.scalar.activation(out=sm[it][:], in_=pt[it][:], func=ACT.Copy, scale=SLOPE)
+                nc.scalar.activation(out=sm[k][:], in_=pt[k][:], func=ACT.Copy, scale=SLOPE)
 
-        def larger(b, ot, half=None):
-            it = (b, ot)
-            js = slice(0, 4) if half is None else slice(2 * half, 2 * half + 2)
-            n = slice(js.start * P, js.stop * P)
-            nc.vector.tensor_tensor(
-                out=osb_of(b, ot)[:, js, :],
-                in0=pt[it][:, n].rearrange("p (j o) -> p j o", o=P),
-                in1=sm[it][:, n].rearrange("p (j o) -> p j o", o=P),
-                op=ALU.max,
-            )
-            if half is None or half == 1:
-                freed.append(ptbank[it])
-
-        def evac(b, ot, on_vector):
-            it = (b, ot)
-            dst = osb_of(b, ot)
-            src = pt[it][:].rearrange("p (j o) -> p j o", j=4)
-            if on_vector:
-                nc.vector.tensor_copy(out=dst, in_=src)
+        def finish(b, h, u, on_vector):
+            k = (b, h, u)
+            dst = osb_of(b, h, u)
+            if (b, 2 * h) not in G_LEAKY:
+                nc.vector.tensor_tensor(out=dst, in0=pt[k][:], in1=sm[k][:], op=ALU.max)
+            elif on_vector:
+                nc.vector.tensor_copy(out=dst, in_=pt[k][:])
             else:
-                nc.scalar.copy(out=dst, in_=src)
-            freed.append(ptbank[it])
-
-        stored = {}
-
-        def done(b, ot):
-            k = (b, ot // 2)
-            if k in SINGLE:
+                nc.scalar.copy(out=dst, in_=pt[k][:])
+            freed.append(ptbank[k])
+            if (b, h) in BY_UNIT:
                 nc.sync.dma_start(
-                    out=out[b].rearrange("(j p) o -> p j o", p=P)[:, :, ot * P:(ot + 1) * P],
-                    in_=osb[k][:, :, (ot % 2) * P:(ot % 2 + 1) * P],
+                    out=out[b].rearrange("(j p) o -> p j o", p=P)[:, 2 * u:2 * u + 2, h * 256:(h + 1) * 256],
+                    in_=osb[(b, h)][:, 2 * u:2 * u + 2, :],
                 )
-                return
-            stored[k] = stored.get(k, 0) + 1
-            if stored[k] == 2:
+            elif u == 1:
                 nc.sync.dma_start(
-                    out=out[b].rearrange("(j p) o -> p j o", p=P)[:, :, (ot // 2) * 256:(ot // 2 + 1) * 256],
-                    in_=osb[k][:],
+                    out=out[b].rearrange("(j p) o -> p j o", p=P)[:, :, h * 256:(h + 1) * 256],
+                    in_=osb[(b, h)][:],
                 )
 
         for t in range(4):
@@ -423,26 +422,48 @@ def tile_yuyipointupdate_pb_kernel(tc, h1_bytes, h1_scale, W2, g2, b2, out):
         par_b(1)
         par_c(1)
 
-        order = [(b, 2 * h + e) for h in range(2) for b in (3, 0, 2, 1) for e in range(2)]
-        n = len(order)
+        n = 2 * len(PAIRS)
+
+        def item(i):
+            b, h = PAIRS[i // 2]
+            return (b, 2 * h + i % 2)
+
+        def unit(i):
+            b, h = PAIRS[i // 2]
+            return (b, h, i % 2)
+
+        for u in range(2):
+            for e in range(2):
+                norm(*item(e), on_vector=((e, u) in VH), halves=(u,))
         for rr in range(-L1, n + L3):
             i = rr + L1
-            if 0 <= i < n:
-                if i % 8 == 2:
-                    norm(2, 2 * (i // 8))
-                    norm(2, 2 * (i // 8) + 1)
-                if order[i][0] != 2:
-                    norm(*order[i], on_vector=(i in VN))
+            if i == 2:
+                for ot in (0, 1):
+                    norm(2, ot)
+                for ot in (0, 1):
+                    if (2, ot) in G_LEAKY:
+                        gleak_a(ot)
+            if i == G2:
+                for ot in (2, 3):
+                    norm(2, ot)
+                for ot in (0, 1):
+                    if (2, ot) in G_LEAKY:
+                        gleak_b(ot)
+                for ot in (0, 1):
+                    if (2, ot) in G_LEAKY:
+                        gleak_c(ot)
+            if 2 <= i < n and item(i)[0] != 2:
+                norm(*item(i), on_vector=(i in VN))
             for par, ot in CHAIN.get(i, ()):
                 (par_a, par_m, par_b, par_c)[par](ot)
             if 0 <= rr + L2 < n:
-                turn(*order[rr + L2])
-            if 0 <= rr < n:
-                small(*order[rr], rr in V_SMALLS)
+                turn(*unit(rr + L2))
+            if 0 <= rr < n and item(rr) not in G_LEAKY:
+                small(*unit(rr), rr in V_SMALLS)
             e = rr - L3
-            if e >= 0:
-                larger(*order[e])
-                done(*order[e])
+            for e in {1: (0, 1), 2: ()}.get(rr, (rr - L3,)) if EARLY else (rr - L3,):
+                if e >= 0:
+                    finish(*unit(e), e in V_SMALLS)
             if rr == RC1:
                 recompute(0, 2)
                 recompute(0, 3)

@@ -33,14 +33,13 @@ VN = (3,)
 CHAIN = {3: ((0, 2), (1, 2), (0, 3), (1, 3)), 4: ((2, 2), (3, 2), (2, 3), (3, 3))}
 V_NORMS = ()
 G_LEAKY = ((2, 0), (2, 1))
-VH = ((1, 0), (1, 1))
 EARLY = False
 G2 = 8
 BY_UNIT = ((3, 0), (0, 0), (2, 1), (0, 1), (1, 0), (3, 1), (2, 0), (1, 1))
-PAIRS = ((3, 0), (0, 0), (1, 0), (3, 1), (2, 1), (0, 1), (2, 0), (1, 1))
-V_SMALLS = (0, 1, 3, 6, 9, 12)
+PAIRS = ((3, 0), (0, 0), (1, 0), (3, 1), (2, 1), (0, 1), (1, 1), (2, 0))
+V_SMALLS = (0, 1, 3, 6, 9, 15)
 P_SHARES = (4, 5, 6)
-PN = 128
+PN = 160
 S_INTERLEAVES = (7,)
 S_WEVAC = True
 P_INTERLEAVES = ()
@@ -59,7 +58,7 @@ def tile_yuyipointupdate_pb_kernel(tc, h1_bytes, h1_scale, W2, g2, b2, out):
         ctx.enter_context(tc.manual_schedule())
 
         hscale = const.tile([P, NG, 8], F32, name="hscale")
-        nc.sync.dma_start(
+        nc.scalar.dma_start(
             out=hscale[:, :, 0:4],
             in_=h1_scale.rearrange("a k u -> (a k u)").rearrange("(g p t) -> p g t", p=P, t=4),
         )
@@ -223,9 +222,9 @@ def tile_yuyipointupdate_pb_kernel(tc, h1_bytes, h1_scale, W2, g2, b2, out):
                 stop=(g == 1),
             )
 
-        def sweep(c):
+        def sweep(c, tiles=range(NOT)):
             b = c // 2
-            for ot in range(NOT):
+            for ot in tiles:
                 if c % 2 == 0:
                     zbank[(b, ot)] = 4 * (b % 2) + ot
                     z[(b, ot)] = bank(zbank[(b, ot)], "z%d%d" % (b, ot))
@@ -376,19 +375,18 @@ def tile_yuyipointupdate_pb_kernel(tc, h1_bytes, h1_scale, W2, g2, b2, out):
             if c not in S_INTERLEAVES:
                 interleave(c)
             quantize(c - 1)
-            sweep(c - 1)
+            sweep(c - 1, range(2) if c == 7 else range(NOT))
             if c + 1 in P_SHARES:
                 interleave_pool(c + 1)
             if 3 <= c < 7:
                 bn(*bn_order[2 * (c - 3)])
                 bn(*bn_order[2 * (c - 3) + 1])
-        tail = [(2, ot) for ot in (0, 1) if ot not in SQ]
-        if len(tail) > 1:
-            bn(*tail[0])
         quantize(7)
-        sweep(7)
-        if tail:
-            bn(*tail[-1])
+        sweep(7, range(2))
+        sweep(6, range(2, NOT))
+        sweep(7, range(2, NOT))
+        bn(2, 0)
+        bn(2, 1)
 
         for ot in (2, 3):
             raw(ot)
@@ -408,19 +406,18 @@ def tile_yuyipointupdate_pb_kernel(tc, h1_bytes, h1_scale, W2, g2, b2, out):
         bn(3, 0)
         bn(3, 1)
         aggr(0)
-        aggr(1)
         bn(3, 2)
+        aggr(1)
         bn(3, 3)
         aggr(2)
         aggr(3)
+
         par_a(0)
         par_m(0)
-        par_a(1)
-        par_m(1)
         par_b(0)
         par_c(0)
-        par_b(1)
-        par_c(1)
+        par_a(1)
+        par_m(1)
 
         n = 2 * len(PAIRS)
 
@@ -432,9 +429,12 @@ def tile_yuyipointupdate_pb_kernel(tc, h1_bytes, h1_scale, W2, g2, b2, out):
             b, h = PAIRS[i // 2]
             return (b, h, i % 2)
 
-        for u in range(2):
-            for e in range(2):
-                norm(*item(e), on_vector=((e, u) in VH), halves=(u,))
+        norm(*item(0), halves=(0,))
+        par_b(1)
+        par_c(1)
+        norm(*item(1), on_vector=True, halves=(0,))
+        norm(*item(0), halves=(1,))
+        norm(*item(1), on_vector=True, halves=(1,))
         for rr in range(-L1, n + L3):
             i = rr + L1
             if i == 2:

@@ -28,17 +28,18 @@ L2 = 2
 L3 = 1
 RC1 = 2
 RC2 = 5
-SQ = (2, 3)
+SQ = (0, 2, 3)
 VN = (3,)
 CHAIN = {3: ((0, 2), (1, 2), (0, 3), (1, 3)), 4: ((2, 2), (3, 2), (2, 3), (3, 3))}
 V_NORMS = ()
 G_LEAKY = ((2, 0), (2, 1))
+RAWS = (0, 2, 3, 1)
 EARLY = False
 G2 = 8
 BY_UNIT = ((3, 0), (0, 0), (2, 1), (0, 1), (1, 0), (3, 1), (2, 0), (1, 1))
 PAIRS = ((3, 0), (0, 0), (1, 0), (3, 1), (2, 1), (0, 1), (1, 1), (2, 0))
 V_SMALLS = (0, 1, 3, 6, 9, 15)
-P_SHARES = (4, 5, 6)
+P_SHARES = (4, 5, 6, 7)
 PN = 160
 S_INTERLEAVES = (7,)
 S_WEVAC = True
@@ -91,6 +92,7 @@ def tile_yuyipointupdate_pb_kernel(tc, h1_bytes, h1_scale, W2, g2, b2, out):
         nc.vector.memset(one[:], 1.0)
         warm = const.tile([P, 1], F32, name="warm")
         nc.scalar.activation(out=warm[:], in_=one[:], func=ACT.Abs_reciprocal_sqrt)
+        go = const.tile([P, 1], F32, name="go")
         ident = const.tile([P, P], F32, name="ident")
         make_identity(nc, ident[:])
         g2pm = const.tile([P, NOT, 2], F32, name="g2pm")
@@ -164,20 +166,24 @@ def tile_yuyipointupdate_pb_kernel(tc, h1_bytes, h1_scale, W2, g2, b2, out):
             grp[c] = grp_pool.tile([P, 4 * NN], BF16, name="grp%d" % c, tag="grpS" if c in S_INTERLEAVES else "grp", bufs=1 if c in S_INTERLEAVES else 2, align_bytes=64)
 
         def interleave_pool(c):
-            new_grp(c)
+            scalar1 = 1.0
+            if c in S_INTERLEAVES:
+                nc.vector.memset(go[:], 1.0)
+                scalar1 = go[:]
             nc.gpsimd.tensor_scalar(
-                out=grp[c][:, 0:4 * PN].rearrange("p (n t) -> p n t", t=4),
-                in0=planes[c][:, :, 0:PN].rearrange("p t n -> p n t"),
-                scalar1=1.0, scalar2=0.0, op0=ALU.mult, op1=ALU.add,
+                out=grp[c][:, 0:4 * PN].rearrange("p (c i t) -> p c t i", i=4, t=4),
+                in0=planes[c][:, :, 0:PN].rearrange("p t (c i) -> p c t i", i=4),
+                scalar1=scalar1, scalar2=0.0, op0=ALU.mult, op1=ALU.add,
             )
+
 
         def interleave(c):
             n0 = PN if c in P_SHARES else 0
-            if c not in P_SHARES:
+            if c not in P_SHARES or c in S_INTERLEAVES:
                 new_grp(c)
             if c in S_INTERLEAVES:
-                dst = grp[c][:, 4 * n0:].rearrange("p (n t) -> p n t", t=4)
-                src = planes[c][:, :, n0:].rearrange("p t n -> p n t")
+                dst = grp[c][:, 4 * n0:].rearrange("p (c i t) -> p c t i", i=4, t=4)
+                src = planes[c][:, :, n0:].rearrange("p t (c i) -> p c t i", i=4)
                 nc.scalar.copy(out=dst, in_=src)
             else:
                 dst = grp[c][:, 4 * n0:].rearrange("p (c i t) -> p c t i", i=4, t=4)
@@ -377,6 +383,8 @@ def tile_yuyipointupdate_pb_kernel(tc, h1_bytes, h1_scale, W2, g2, b2, out):
             quantize(c - 1)
             sweep(c - 1, range(2) if c == 7 else range(NOT))
             if c + 1 in P_SHARES:
+                if c + 1 not in S_INTERLEAVES:
+                    new_grp(c + 1)
                 interleave_pool(c + 1)
             if 3 <= c < 7:
                 bn(*bn_order[2 * (c - 3)])
@@ -385,22 +393,22 @@ def tile_yuyipointupdate_pb_kernel(tc, h1_bytes, h1_scale, W2, g2, b2, out):
         sweep(7, range(2))
         sweep(6, range(2, NOT))
         sweep(7, range(2, NOT))
-        bn(2, 0)
-        bn(2, 1)
+        for ot in range(2):
+            if ot not in SQ:
+                bn(2, ot)
 
-        for ot in (2, 3):
-            raw(ot)
-            square(ot)
-            free_z2(ot)
-        triple(2, 3)
-        recompute(0, 0)
-        recompute(0, 1)
-        for ot in (0, 1):
+        for ot in RAWS:
             raw(ot)
             if ot in SQ:
                 square(ot)
-                triple(ot, ot)
             free_z2(ot)
+            if ot == 0 and 0 in SQ:
+                triple(0, 0)
+            if ot == 3:
+                triple(2, 3)
+            if ot == RAWS[1]:
+                recompute(0, 0)
+                recompute(0, 1)
         recompute(1, 0)
         recompute(1, 1)
         bn(3, 0)

from contextlib import ExitStack

import concourse.mybir as mybir
from concourse.masks import make_identity

FLOPS = 2 * 512 * 1024 * 2048

F32 = mybir.dt.float32
BF16 = mybir.dt.bfloat16
U32 = mybir.dt.uint32
U8 = mybir.dt.uint8
FP8 = mybir.dt.float8_e4m3fn
FP8X4 = mybir.dt.float8_e4m3fn_x4
ACT = mybir.ActivationFunctionType
ALU = mybir.AluOpType

P = 128
NB = 4
NN = 512
NOT = 4
NG = 2
EPS = 1e-5
SLOPE = 0.01

V_WIDENS = ((0, 1), (0, 2), (0, 3), (1, 3), (2, 2), (2, 3), (3, 3))
L1 = 4
L2 = 2
L3 = 1
RC1 = 2
RC2 = 5
SQ = (0, 2, 3)
VN = (3,)
CHAIN = {3: ((0, 2), (1, 2), (0, 3), (1, 3)), 4: ((2, 2), (3, 2), (2, 3), (3, 3))}
V_NORMS = ()
G_LEAKY = ((2, 0), (2, 1))
RAWS = (0, 2, 3, 1)
EARLY = False
G2 = 8
BY_UNIT = ((3, 0), (0, 0), (2, 1), (0, 1), (1, 0), (3, 1), (2, 0), (1, 1))
PAIRS = ((3, 0), (0, 0), (1, 0), (3, 1), (2, 1), (0, 1), (1, 1), (2, 0))
V_SMALLS = (0, 1, 3, 6, 9, 15)
P_SHARES = (4, 5, 6, 7)
PN = 160
S_INTERLEAVES = (7,)
S_WEVAC = True
P_INTERLEAVES = ()
P_NORMS = False


def tile_yuyipointupdate_pb_kernel(tc, h1_bytes, h1_scale, W2, g2, b2, out):
    nc = tc.nc
    with ExitStack() as ctx:
        const = ctx.enter_context(tc.tile_pool(name="const", bufs=1))
        keep = ctx.enter_context(tc.tile_pool(name="keep", bufs=1))
        grp_pool = ctx.enter_context(tc.tile_pool(name="grp", bufs=4))
        yr_pool = ctx.enter_context(tc.tile_pool(name="yr", bufs=4))
        o_pool = ctx.enter_context(tc.tile_pool(name="osb", bufs=8))
        psum = ctx.enter_context(tc.psum_pool(name="psum", bufs=1))
        ctx.enter_context(tc.manual_schedule())

        hscale = const.tile([P, NG, 8], F32, name="hscale")
        nc.scalar.dma_start(
            out=hscale[:, :, 0:4],
            in_=h1_scale.rearrange("a k u -> (a k u)").rearrange("(g p t) -> p g t", p=P, t=4),
        )
        hb = []
        for c in range(8):
            hb.append(keep.tile([P, 4, NN], U8, name="hbytes%d" % c))
        wraw = []
        for ot in range(NOT):
            wraw.append(keep.tile([P, 1024], BF16, name="wraw%d" % ot))

        def load_h(c):
            b, g = c // 2, c % 2
            nc.sync.dma_start(out=hb[c][:], in_=h1_bytes[b].rearrange("(g p t) n -> g p t n", p=P, t=4)[g])

        for half in range(2):
            ts = slice(2 * half, 2 * half + 2)
            nc.sync.dma_start(out=hb[0][:, ts, :], in_=h1_bytes[0].rearrange("(g p t) n -> g p t n", p=P, t=4)[0][:, ts, :])
        load_h(1)
        for ot in range(NOT):
            nc.sync.dma_start(out=wraw[ot][:], in_=W2[ot * P:(ot + 1) * P, :])
        for c in range(2, 8):
            load_h(c)
        g2raw = const.tile([P, NOT, 1], BF16, name="g2raw")
        b2raw = const.tile([P, NOT, 1], BF16, name="b2raw")
        with nc.allow_non_contiguous_dma(reason="512 gains and shifts, one to a partition and tile"):
            nc.sync.dma_start(out=g2raw[:].rearrange("p t u -> p (t u)"), in_=g2.rearrange("(t p) -> p t", p=P))
            nc.sync.dma_start(out=b2raw[:].rearrange("p t u -> p (t u)"), in_=b2.rearrange("(t p) -> p t", p=P))

        one = const.tile([P, 1], F32, name="one")
        nc.vector.memset(one[:], 1.0)
        warm = const.tile([P, 1], F32, name="warm")
        nc.scalar.activation(out=warm[:], in_=one[:], func=ACT.Abs_reciprocal_sqrt)
        go = const.tile([P, 1], F32, name="go")
        ident = const.tile([P, P], F32, name="ident")
        make_identity(nc, ident[:])
        g2pm = const.tile([P, NOT, 2], F32, name="g2pm")
        b2f = const.tile([P, NOT, 1], F32, name="b2f")
        nc.gpsimd.tensor_copy(out=g2pm[:, :, 0:1], in_=g2raw[:])
        nc.gpsimd.tensor_scalar(out=g2pm[:, :, 1:2], in0=g2raw[:], scalar1=-1.0, scalar2=0.0, op0=ALU.mult, op1=ALU.add)
        nc.gpsimd.tensor_copy(out=b2f[:], in_=b2raw[:])

        planes = []
        hcod = []
        hscl = []
        for c in range(8):
            planes.append(keep.tile([P, 4, NN], BF16, name="planes%d" % c))
            hcod.append(keep.tile([P, NN], U32, name="hcod%d" % c, align_bytes=64))
            hscl.append(keep.tile([P, NN], U8, name="hscl%d" % c, align_bytes=64))
        wgrp = []
        wcod = []
        wscl = []
        for g in range(NG):
            wgrp.append(keep.tile([P, 2048], BF16, name="wgrp%d" % g, align_bytes=64))
            wcod.append(keep.tile([P, 512], U32, name="wcod%d" % g, align_bytes=64))
            wscl.append(keep.tile([P, 512], U8, name="wscl%d" % g, align_bytes=64))
        stats = const.tile([P, NOT, 32], F32, name="stats")
        sums = const.tile([P, NOT, 1], F32, name="sums")
        sqs = const.tile([P, NOT, 1], F32, name="sqs")
        m2 = const.tile([P, NOT, 1], F32, name="m2")
        junk = const.tile([P, NN], F32, name="junk")
        nc.gpsimd.memset(stats[:, :, 5:6], float(NN))
        mv = const.tile([P, NOT, 2], F32, name="mv")
        rstd = const.tile([P, NOT, 1], F32, name="rstd")
        gg = const.tile([P, NOT, 1], F32, name="gg")
        mg = const.tile([P, NOT, 1], F32, name="mg")
        shift = const.tile([P, NOT, 1], F32, name="shift")
        grp = {}
        xt = {}
        z = {}
        zbank = {}
        zs = {}
        y = {}
        r = {}
        pt = {}
        ptbank = {}
        osb = {}
        freed = []
        taken = [0]
        gt = {}
        gu = {}
        sm = {}

        bn_order = [(b, ot) for b in range(3) for ot in range(NOT)]

        def bank(k, name):
            return psum.tile([P, NN], F32, name=name, tag="bank%d" % k)

        def take():
            k = freed[taken[0]]
            taken[0] += 1
            return k

        def widen(c, t):
            g = c % 2
            src = hb[c][:, t, :].bitcast(FP8)
            dst = planes[c][:, t, :]
            sc = hscale[:, g, t:t + 1]
            if (c, t) in V_WIDENS:
                nc.vector.tensor_scalar(out=dst, in0=src, scalar1=sc, scalar2=None, op0=ALU.mult)
            else:
                nc.scalar.activation(out=dst, in_=src, func=ACT.Copy, scale=sc)

        def new_grp(c):
            grp[c] = grp_pool.tile([P, 4 * NN], BF16, name="grp%d" % c, tag="grpS" if c in S_INTERLEAVES else "grp", bufs=1 if c in S_INTERLEAVES else 2, align_bytes=64)

        def interleave_pool(c):
            scalar1 = 1.0
            if c in S_INTERLEAVES:
                nc.vector.memset(go[:], 1.0)
                scalar1 = go[:]
            nc.gpsimd.tensor_scalar(
                out=grp[c][:, 0:4 * PN].rearrange("p (c i t) -> p c t i", i=4, t=4),
                in0=planes[c][:, :, 0:PN].rearrange("p t (c i) -> p c t i", i=4),
                scalar1=scalar1, scalar2=0.0, op0=ALU.mult, op1=ALU.add,
            )


        def interleave(c):
            n0 = PN if c in P_SHARES else 0
            if c not in P_SHARES or c in S_INTERLEAVES:
                new_grp(c)
            if c in S_INTERLEAVES:
                dst = grp[c][:, 4 * n0:].rearrange("p (c i t) -> p c t i", i=4, t=4)
                src = planes[c][:, :, n0:].rearrange("p t (c i) -> p c t i", i=4)
                nc.scalar.copy(out=dst, in_=src)
            else:
                dst = grp[c][:, 4 * n0:].rearrange("p (c i t) -> p c t i", i=4, t=4)
                src = planes[c][:, :, n0:].rearrange("p t (c i) -> p c t i", i=4)
                nc.vector.tensor_copy(out=dst, in_=src)

        def quantize(c):
            nc.vector.quantize_mx(out=hcod[c][:].bitcast(FP8X4), scales=hscl[c][:], in_=grp[c][:])

        def w_transposes(h, g):
            xt[(h, g)] = bank(4 + 2 * h + g, "xt%d%d" % (h, g))
            for u in range(2):
                for otl in range(2):
                    words = wraw[2 * h + otl][:].bitcast(F32)
                    nc.tensor.transpose(
                        xt[(h, g)][:, u * 256 + otl * P:u * 256 + (otl + 1) * P],
                        words[:, 256 * g + u:256 * (g + 1):2],
                        ident[:],
                    )

        def w_evac(h, g):
            dst = wgrp[g][:].bitcast(F32)[:, h * 512:(h + 1) * 512].rearrange("p (r u) -> p r u", u=2)
            src = xt[(h, g)][:].rearrange("p (u r) -> p r u", u=2)
            if S_WEVAC:
                nc.scalar.copy(out=dst, in_=src)
            else:
                nc.vector.tensor_copy(out=dst, in_=src)

        def w_quantize(g):
            nc.vector.quantize_mx(out=wcod[g][:].bitcast(FP8X4), scales=wscl[g][:], in_=wgrp[g][:])

        def mx(acc, ot, c):
            g = c % 2
            cols = slice(ot * P, (ot + 1) * P)
            nc.tensor.matmul_mx(
                out=acc[:],
                lhsT=wcod[g][:, cols].bitcast(FP8X4),
                lhsT_scale=wscl[g][:, cols],
                rhs=hcod[c][:].bitcast(FP8X4),
                rhs_scale=hscl[c][:],
                start=(g == 0),
                stop=(g == 1),
            )

        def sweep(c, tiles=range(NOT)):
            b = c // 2
            for ot in tiles:
                if c % 2 == 0:
                    zbank[(b, ot)] = 4 * (b % 2) + ot
                    z[(b, ot)] = bank(zbank[(b, ot)], "z%d%d" % (b, ot))
                mx(z[(b, ot)], ot, c)

        def bn(b, ot):
            col = {0: 8, 1: 14, 3: 20, 2: 26}[b]
            nc.vector.bn_stats(out=stats[:, ot, col:col + 6], in_=z[(b, ot)][:])

        def aggr(ot):
            nc.vector.bn_aggr(out=mv[:, ot, :], in_=stats[:, ot, 5:26] if ot in SQ else stats[:, ot, 8:32])

        def par_a(ot):
            nc.scalar.activation(out=rstd[:, ot, :], in_=mv[:, ot, 1:2], func=ACT.Abs_reciprocal_sqrt, bias=EPS, scale=1.0)

        def par_m(ot):
            nc.scalar.activation(out=mg[:, ot, :], in_=mv[:, ot, 0:1], func=ACT.Copy, scale=g2pm[:, ot, 1:2])

        def par_b(ot):
            nc.scalar.activation(out=gg[:, ot, :], in_=g2pm[:, ot, 0:1], func=ACT.Copy, scale=rstd[:, ot, :])

        def par_c(ot):
            nc.scalar.activation(out=shift[:, ot, :], in_=mg[:, ot, :], func=ACT.Identity, bias=b2f[:, ot, :], scale=rstd[:, ot, :])

        def raw(ot):
            zs[ot] = keep.tile([P, NN], F32, name="zs%d" % ot)
            if ot in SQ:
                nc.scalar.activation(out=zs[ot][:], in_=z[(2, ot)][:], func=ACT.Copy, accum_out=sums[:, ot, :])
            else:
                nc.scalar.copy(out=zs[ot][:], in_=z[(2, ot)][:])

        def square(ot):
            nc.scalar.activation(out=junk[:], in_=z[(2, ot)][:], func=ACT.Square, accum_out=sqs[:, ot, :])

        def triple(first, last):
            ots = slice(first, last + 1)
            nc.gpsimd.tensor_scalar(out=stats[:, ots, 6:7], in0=sums[:, ots, :], scalar1=1.0 / NN, scalar2=0.0, op0=ALU.mult, op1=ALU.add)
            nc.gpsimd.tensor_tensor(out=m2[:, ots, :], in0=sums[:, ots, :], in1=stats[:, ots, 6:7], op=ALU.mult)
            nc.gpsimd.tensor_tensor(out=stats[:, ots, 7:8], in0=sqs[:, ots, :], in1=m2[:, ots, :], op=ALU.subtract)

        def free_z2(ot):
            freed.append(zbank[(2, ot)])

        def recompute(b, ot):
            zbank[(b, ot)] = take()
            z[(b, ot)] = bank(zbank[(b, ot)], "zz%d%d" % (b, ot))
            mx(z[(b, ot)], ot, 2 * b)
            mx(z[(b, ot)], ot, 2 * b + 1)

        def norm(b, ot, on_vector=False, halves=(0, 1)):
            it = (b, ot)
            if it not in y:
                y[it] = yr_pool.tile([P, NN], F32, name="y%d%d" % it, tag="yp" if b == 2 else "y", bufs=4 if b == 2 else 8)
            cols = slice(halves[0] * 256, halves[-1] * 256 + 256)
            dst = y[it][:, cols]
            if b == 2:
                nc.gpsimd.tensor_scalar(out=dst, in0=zs[ot][:, cols], scalar1=gg[:, ot, 0:1], scalar2=shift[:, ot, :], op0=ALU.mult, op1=ALU.add)
                return
            if on_vector:
                nc.vector.tensor_scalar(out=dst, in0=z[it][:, cols], scalar1=gg[:, ot, 0:1], scalar2=shift[:, ot, :], op0=ALU.mult, op1=ALU.add)
            else:
                nc.scalar.activation(out=dst, in_=z[it][:, cols], func=ACT.Identity, bias=shift[:, ot, :], scale=gg[:, ot, 0:1])
            if halves[-1] == 1:
                freed.append(zbank[it])

        def gleak_a(ot):
            gt[ot] = yr_pool.tile([P, NN], F32, name="gt%d" % ot, tag="gt", bufs=2)
            nc.gpsimd.tensor_scalar(out=gt[ot][:], in0=y[(2, ot)][:], scalar1=0.0, scalar2=None, op0=ALU.min)

        def gleak_b(ot):
            gu[ot] = yr_pool.tile([P, NN], F32, name="gu%d" % ot, tag="gu", bufs=2)
            nc.gpsimd.tensor_scalar(out=gu[ot][:], in0=gt[ot][:], scalar1=SLOPE - 1.0, scalar2=0.0, op0=ALU.mult, op1=ALU.add)

        def gleak_c(ot):
            r[(2, ot)] = yr_pool.tile([P, NN], F32, name="gr%d" % ot, tag="gr", bufs=2)
            nc.gpsimd.tensor_tensor(out=r[(2, ot)][:], in0=y[(2, ot)][:], in1=gu[ot][:], op=ALU.add)

        def turn(b, h, u):
            k = (b, h, u)
            ptbank[k] = take()
            pt[k] = bank(ptbank[k], "pt%d%d%d" % k)
            for j in range(2):
                for e in range(2):
                    it = (b, 2 * h + e)
                    src = r[it] if it in G_LEAKY else y[it]
                    nc.tensor.transpose(
                        pt[k][:, (2 * j + e) * P:(2 * j + e + 1) * P],
                        src[:, (2 * u + j) * P:(2 * u + j + 1) * P],
                        ident[:],
                    )

        def osb_of(b, h, u):
            if (b, h) not in osb:
                osb[(b, h)] = o_pool.tile([P, 4, 256], F32, name="osb%d%d" % (b, h), tag="osb")
            return osb[(b, h)][:, 2 * u:2 * u + 2, :].rearrange("p j o -> p (j o)")

        def small(b, h, u, on_vector):
            k = (b, h, u)
            sm[k] = yr_pool.tile([P, NN], F32, name="sm%d%d%d" % k, tag="smV" if on_vector else "sm", bufs=4)
            if on_vector:
                nc.vector.tensor_scalar(out=sm[k][:], in0=pt[k][:], scalar1=SLOPE, scalar2=None, op0=ALU.mult)
            else:
                nc.scalar.activation(out=sm[k][:], in_=pt[k][:], func=ACT.Copy, scale=SLOPE)

        def finish(b, h, u, on_vector):
            k = (b, h, u)
            dst = osb_of(b, h, u)
            if (b, 2 * h) not in G_LEAKY:
                nc.vector.tensor_tensor(out=dst, in0=pt[k][:], in1=sm[k][:], op=ALU.max)
            elif on_vector:
                nc.vector.tensor_copy(out=dst, in_=pt[k][:])
            else:
                nc.scalar.copy(out=dst, in_=pt[k][:])
            freed.append(ptbank[k])
            if (b, h) in BY_UNIT:
                nc.sync.dma_start(
                    out=out[b].rearrange("(j p) o -> p j o", p=P)[:, 2 * u:2 * u + 2, h * 256:(h + 1) * 256],
                    in_=osb[(b, h)][:, 2 * u:2 * u + 2, :],
                )
            elif u == 1:
                nc.sync.dma_start(
                    out=out[b].rearrange("(j p) o -> p j o", p=P)[:, :, h * 256:(h + 1) * 256],
                    in_=osb[(b, h)][:],
                )

        for t in range(4):
            widen(0, t)
        for t in range(4):
            widen(1, t)
        for h in range(2):
            for g in range(NG):
                w_transposes(h, g)
        interleave(0)
        interleave(1)
        for h in range(2):
            for g in range(NG):
                w_evac(h, g)
        quantize(0)
        for c in range(2, 8):
            for t in range(4):
                widen(c, t)
            if c in S_INTERLEAVES:
                interleave(c)
        w_quantize(0)
        sweep(0)
        w_quantize(1)
        for c in range(2, 8):
            if c not in S_INTERLEAVES:
                interleave(c)
            quantize(c - 1)
            sweep(c - 1, range(2) if c == 7 else range(NOT))
            if c + 1 in P_SHARES:
                if c + 1 not in S_INTERLEAVES:
                    new_grp(c + 1)
                interleave_pool(c + 1)
            if 3 <= c < 7:
                bn(*bn_order[2 * (c - 3)])
                bn(*bn_order[2 * (c - 3) + 1])
        quantize(7)
        sweep(7, range(2))
        sweep(6, range(2, NOT))
        sweep(7, range(2, NOT))
        for ot in range(2):
            if ot not in SQ:
                bn(2, ot)

        for ot in RAWS:
            raw(ot)
            if ot in SQ:
                square(ot)
            free_z2(ot)
            if ot == 0 and 0 in SQ:
                triple(0, 0)
            if ot == 3:
                triple(2, 3)
            if ot == RAWS[1]:
                recompute(0, 0)
                recompute(0, 1)
        recompute(1, 0)
        recompute(1, 1)
        bn(3, 0)
        bn(3, 1)
        aggr(0)
        bn(3, 2)
        aggr(1)
        bn(3, 3)
        aggr(2)
        aggr(3)

        par_a(0)
        par_m(0)
        par_b(0)
        par_c(0)
        par_a(1)
        par_m(1)

        n = 2 * len(PAIRS)

        def item(i):
            b, h = PAIRS[i // 2]
            return (b, 2 * h + i % 2)

        def unit(i):
            b, h = PAIRS[i // 2]
            return (b, h, i % 2)

        norm(*item(0), halves=(0,))
        par_b(1)
        par_c(1)
        norm(*item(1), on_vector=True, halves=(0,))
        norm(*item(0), halves=(1,))
        norm(*item(1), on_vector=True, halves=(1,))
        for rr in range(-L1, n + L3):
            i = rr + L1
            if i == 2:
                for ot in (0, 1):
                    norm(2, ot)
                for ot in (0, 1):
                    if (2, ot) in G_LEAKY:
                        gleak_a(ot)
            if i == G2:
                for ot in (2, 3):
                    norm(2, ot)
                for ot in (0, 1):
                    if (2, ot) in G_LEAKY:
                        gleak_b(ot)
                for ot in (0, 1):
                    if (2, ot) in G_LEAKY:
                        gleak_c(ot)
            if 2 <= i < n and item(i)[0] != 2:
                norm(*item(i), on_vector=(i in VN))
            for par, ot in CHAIN.get(i, ()):
                (par_a, par_m, par_b, par_c)[par](ot)
            if 0 <= rr + L2 < n:
                turn(*unit(rr + L2))
            if 0 <= rr < n and item(rr) not in G_LEAKY:
                small(*unit(rr), rr in V_SMALLS)
            e = rr - L3
            for e in {1: (0, 1), 2: ()}.get(rr, (rr - L3,)) if EARLY else (rr - L3,):
                if e >= 0:
                    finish(*unit(e), e in V_SMALLS)
            if rr == RC1:
                recompute(0, 2)
                recompute(0, 3)
            if rr == RC2:
                recompute(1, 2)
                recompute(1, 3)
